import numpy as np
import ml_dtypes


def mxq(x, axis, fmt="e4m3"):
    dtype, down = {"e4m3": (ml_dtypes.float8_e4m3fn, 7), "e5m2": (ml_dtypes.float8_e5m2, 14)}[fmt]
    v = np.moveaxis(np.asarray(x, np.float32).astype(ml_dtypes.bfloat16).astype(np.float64), axis, -1)
    blocks = v.reshape(v.shape[:-1] + (-1, 32))
    amax = np.abs(blocks).max(-1, keepdims=True)
    byte = np.maximum(np.where(amax > 0, np.frexp(amax)[1] - 1 + 127, 0) - down, 1)
    scale = np.exp2(byte - 127.0)
    codes = (blocks / scale).astype(np.float32).astype(dtype).astype(np.float64)
    return np.moveaxis((codes * scale).reshape(v.shape), -1, axis)


WIDE = False


def mx_kscale(k):
    if not WIDE:
        return np.ones(k)
    levels = np.array([10, -10, 5, -5, 0])
    if k % 512:
        return np.exp2(np.random.permutation(np.resize(levels, k // 32))).repeat(32)
    a = np.empty((k // 512, 16))
    for p in range(k // 512):
        a[p, :8] = np.random.permutation(np.resize(levels, 8))
        for g in range(8):
            far = levels[np.abs(levels - a[p, g]) >= 10]
            a[p, g + 8] = far[np.random.randint(len(far))]
    return np.exp2(a.ravel()).repeat(32)


BF16 = ml_dtypes.bfloat16


def bf(x):
    return np.asarray(x, np.float32).astype(BF16)


def f64(x):
    return np.asarray(x).astype(np.float64)


B, D_IN, D_HID, SHARE = 4096, 1024, 128, 2
NUM_GATE = 4 + SHARE


def sigmoid(v):
    return 1.0 / (1.0 + np.exp(-v))


def setup_inputs():
    s = mx_kscale(D_IN)
    n = np.random.standard_normal
    return {
        "input": bf(n((B, D_IN)) * s),
        "h_minors": bf(n((B, D_HID))),
        "c_minors": bf(n((B, D_HID))),
        "s_minors": bf(n((SHARE, B, D_HID))),
        "mask": bf(np.random.uniform(0.5, 1.5, B)),
        "weight_ih": bf(n((NUM_GATE * D_HID, D_IN)) * 0.7 / np.sqrt(D_IN) / s),
        "weight_hh": bf(n((4 * D_HID, D_HID)) * 0.7 / np.sqrt(D_HID)),
        "weight_sh": bf(n((SHARE * D_HID, D_HID)) * 0.7 / np.sqrt(D_HID)),
        "bias_ih": bf(n(NUM_GATE * D_HID) * 0.3),
        "bias_hh": bf(n(4 * D_HID) * 0.3),
        "bias_sh": bf(n(SHARE * D_HID) * 0.3),
        "idx": 0,
    }


def reference(input, h_minors, c_minors, s_minors, mask, weight_ih, weight_hh, weight_sh, bias_ih, bias_hh, bias_sh, idx):
    H = weight_hh.shape[1]
    share = weight_sh.shape[0] // H
    m = f64(mask)[:, None]
    tmp = (mxq(f64(input), 1, "e4m3") @ mxq(f64(weight_ih), 1, "e4m3").T) + f64(bias_ih)
    tmp2 = f64(h_minors) @ f64(weight_hh).T + f64(bias_hh)
    tmp3 = f64(s_minors)[idx] @ f64(weight_sh).T + f64(bias_sh)
    tmp_in, tmp_s = tmp[:, :4 * H], tmp[:, 4 * H:]
    z = tmp_in + tmp2
    ifo = sigmoid(z[:, :3 * H])
    i, f, o = ifo[:, :H], ifo[:, H:2 * H], ifo[:, 2 * H:]
    c_hat = z[:, 3 * H:]
    b = sigmoid(tmp_s + tmp3)
    c_t = (f * f64(c_minors) + i * np.tanh(c_hat)) * m
    tc = np.tanh(c_t) * m
    h = o * tc
    s = b.reshape(-1, share, H) * tc[:, None, :]
    s = np.moveaxis(s, 1, 0)
    return (h, c_t, s[0], s[1])

@@ -1,0 +1,415 @@
+from contextlib import ExitStack
+
+import concourse.mybir as mybir
+from concourse.masks import make_identity
+
+F32 = mybir.dt.float32
+BF16 = mybir.dt.bfloat16
+U32 = mybir.dt.uint32
+U8 = mybir.dt.uint8
+FP8X4 = mybir.dt.float8_e4m3fn_x4
+ACT = mybir.ActivationFunctionType
+ALU = mybir.AluOpType
+
+P = 128
+B = 4096
+D_IN = 1024
+H = 128
+NG = 768
+NT = B // P
+NPAIR = NT // 2
+NGROUP = NT // 4
+LA = 1
+XL = 3
+QL = 2
+PINNED = True
+NG_SUM = 7
+NG_OUT = 5
+
+FLOPS = 2 * B * (D_IN * NG + H * 512 + H * 256)
+BYTES = 2 * (B * D_IN + 3 * B * H + B + NG * D_IN + 768 * H + 2 * NG) + 4 * 4 * B * H
+
+
+def tile_share_lstm_cell_t_kernel(
+    tc, x_in, h_minors, c_minors, s_minors, mask, weight_ih, weight_hh, weight_sh,
+    bias_ih, bias_hh, bias_sh, idx, out_0, out_1, out_2, out_3,
+):
+    nc = tc.nc
+    with ExitStack() as ctx:
+        const = ctx.enter_context(tc.tile_pool(name="const", bufs=1))
+        xpool = ctx.enter_context(tc.tile_pool(name="xpool", bufs=8))
+        qpool = ctx.enter_context(tc.tile_pool(name="qpool", bufs=3))
+        pbpool = ctx.enter_context(tc.tile_pool(name="pbpool", bufs=LA + 1))
+        gpool = ctx.enter_context(tc.tile_pool(name="gpool", bufs=5))
+        opool = ctx.enter_context(tc.tile_pool(name="opool", bufs=3))
+        psum = ctx.enter_context(tc.psum_pool(name="psum", bufs=1))
+        if PINNED:
+            ctx.enter_context(tc.manual_schedule())
+
+        xv = x_in.rearrange("(p t) k -> p t k", t=NT)
+        hv = h_minors.rearrange("(p t) k -> p t k", t=NT)
+        cv = c_minors.rearrange("(p t) k -> p t k", t=NT)
+        sv = s_minors[idx].rearrange("(p t) k -> p t k", t=NT)
+        wv = weight_ih.rearrange("(j p) k -> p j k", p=P)
+        outs = [o.rearrange("(p t) k -> p t k", t=NT) for o in (out_0, out_1, out_2, out_3)]
+
+        whh_raw = const.tile([P, 6, H], BF16)
+        braw = const.tile([P, NG], BF16)
+        m_bf = const.tile([P, NT], BF16)
+        m32 = const.tile([P, NT], F32)
+        w_raw = const.tile([P, 6, D_IN], BF16)
+        h_sb = const.tile([P, NT, H], BF16)
+        s_sb = const.tile([P, NT, H], BF16)
+        c_sb = const.tile([P, NT, H], BF16)
+        ident_f = const.tile([P, P], F32)
+        ident_b = const.tile([P, P], BF16)
+        ones = const.tile([P, P], BF16)
+        wT = const.tile([P, NG], BF16)
+        bias_bc = const.tile([P, NG], F32)
+        hsT = const.tile([P, NGROUP, 2, 4, H], BF16)
+        w_grp = const.tile([P, 2, NG, 2], F32, align_bytes=64)
+        w_codes = const.tile([P, 2 * NG], U32, align_bytes=64)
+        w_scales = const.tile([P, 2 * NG], U8, align_bytes=64)
+
+        xp_t = {}
+        ps_t = {}
+        xg_t = {}
+        xq_t = {}
+        pb_t = {}
+        g4_t = {}
+        out_t = {}
+
+        def load_x(k):
+            x_sb = xpool.tile([P, 2, D_IN], BF16, name="x_sb")
+            nc.sync.dma_start(out=x_sb[:], in_=xv[:, 2 * k:2 * k + 2, :])
+            xp_t[k] = x_sb
+
+        def copy_out(eng, out, in_):
+            if eng == "V":
+                nc.vector.tensor_copy(out=out, in_=in_)
+            else:
+                nc.scalar.copy(out=out, in_=in_)
+
+        nc.vector.memset(braw[:], 0.0)
+        nc.vector.memset(ones[:], 1.0)
+        make_identity(nc, ident_b[:])
+        make_identity(nc, ident_f[:])
+        nc.scalar.dma_start(out=braw[0:1, :], in_=bias_ih.unsqueeze(0))
+        nc.scalar.dma_start(out=braw[1:2, 0:512], in_=bias_hh.unsqueeze(0))
+        nc.scalar.dma_start(out=braw[1:2, 512:768], in_=bias_sh.unsqueeze(0))
+        nc.sync.dma_start(out=whh_raw[:, 0:4, :], in_=weight_hh.rearrange("(j p) k -> p j k", p=P))
+        nc.sync.dma_start(out=whh_raw[:, 4:6, :], in_=weight_sh.rearrange("(j p) k -> p j k", p=P))
+        nc.sync.dma_start(out=h_sb[:, 0:8, :], in_=hv[:, 0:8, :])
+        nc.sync.dma_start(out=s_sb[:, 0:8, :], in_=sv[:, 0:8, :])
+        nc.sync.dma_start(out=w_raw[:, 0:2, :], in_=wv[:, 0:2, :])
+        nc.sync.dma_start(out=w_raw[:, 2:4, :], in_=wv[:, 2:4, :])
+        load_x(0)
+        nc.sync.dma_start(out=w_raw[:, 4:6, :], in_=wv[:, 4:6, :])
+        load_x(1)
+        nc.scalar.dma_start(out=m_bf[:], in_=mask.rearrange("(p t) -> p t", t=NT))
+        load_x(2)
+        nc.sync.dma_start(out=h_sb[:, 8:NT, :], in_=hv[:, 8:NT, :])
+        nc.sync.dma_start(out=s_sb[:, 8:NT, :], in_=sv[:, 8:NT, :])
+        load_x(3)
+        nc.sync.dma_start(out=c_sb[:], in_=cv)
+        for k in range(4, 8):
+            load_x(k)
+
+        def hs_pe(gi, tag):
+            hs_ps = psum.tile([P, 2, 4, H], BF16, tag=tag, name="hs_ps")
+            ps_t["hs", gi] = hs_ps
+            for tt in range(4):
+                nc.tensor.transpose(hs_ps[:, 0, tt, :], h_sb[:, 4 * gi + tt, :], ident_b[:])
+            for tt in range(4):
+                nc.tensor.transpose(hs_ps[:, 1, tt, :], s_sb[:, 4 * gi + tt, :], ident_b[:])
+
+        def hs_ev(gi, eng):
+            copy_out(eng, hsT[:, gi], ps_t["hs", gi][:])
+
+        def w_pe(j, tag):
+            w_ps = psum.tile([P, 4, P], F32, tag=tag, name="w_ps")
+            ps_t["w", j] = w_ps
+            ww = w_raw[:, j, :].bitcast(F32)
+            for q in range(4):
+                nc.tensor.transpose(w_ps[:, q, :], ww[:, 256 * (q // 2) + q % 2:256 * (q // 2) + 256:2], ident_f[:])
+
+        def w_ev(j, eng):
+            copy_out(eng, w_grp[:, :, P * j:P * j + P, :], ps_t["w", j][:].rearrange("p (g u) r -> p g r u", g=2))
+
+        def w_quant(a):
+            for g in range(2):
+                lo = g * NG + 256 * a
+                nc.vector.quantize_mx(
+                    out=w_codes[:, lo:lo + 256].bitcast(FP8X4), scales=w_scales[:, lo:lo + 256],
+                    in_=w_grp[:, g, 256 * a:256 * a + 256, :].rearrange("p n u -> p (n u)").bitcast(BF16),
+                )
+
+        def x_pe(t, tag):
+            xt = psum.tile([P, 4, P], F32, tag=tag, name="xt")
+            ps_t["x", t] = xt
+            xw = xp_t[t // 2][:, t % 2, :].bitcast(F32)
+            for q in range(4):
+                nc.tensor.transpose(xt[:, q, :], xw[:, 256 * (q // 2) + q % 2:256 * (q // 2) + 256:2], ident_f[:])
+
+        def x_ev(t, eng):
+            k = t // 2
+            if t % 2 == 0:
+                xg_new = qpool.tile([P, 2, 2, P, 2], F32, align_bytes=64, name="xg")
+                xg_t[k] = xg_new
+            copy_out(eng, xg_t[k][:, t % 2], ps_t["x", t][:].rearrange("p (g u) r -> p g r u", g=2))
+
+        def quantise(k):
+            xc = qpool.tile([P, 512], U32, align_bytes=64, name="xc")
+            xs = qpool.tile([P, 512], U8, align_bytes=64, name="xs")
+            xq_t[k] = (xc, xs)
+            nc.vector.quantize_mx(
+                out=xc[:].bitcast(FP8X4), scales=xs[:],
+                in_=xg_t[k][:].rearrange("p t g r u -> p (t g r u)").bitcast(BF16),
+            )
+
+        def plain(k):
+            gi = k // 2
+            tt = 2 * (k % 2)
+            p0 = psum.tile([P, 512], F32, tag="P0", name="p0")
+            p1 = psum.tile([P, 512], F32, tag="P1", name="p1")
+            pc = psum.tile([P, 512], F32, tag="PC", name="pc")
+            ps_t["pl", k] = (p0, p1, pc)
+            nc.tensor.matmul(out=p0[:], lhsT=hsT[:, gi, 0, tt, :], rhs=wT[:, 0:512], start=True, stop=True)
+            nc.tensor.matmul(out=p1[:], lhsT=hsT[:, gi, 0, tt + 1, :], rhs=wT[:, 0:512], start=True, stop=True)
+            nc.tensor.matmul(out=pc[:, 0:256], lhsT=hsT[:, gi, 1, tt, :], rhs=wT[:, 512:768], start=True, stop=True)
+            nc.tensor.matmul(out=pc[:, 256:512], lhsT=hsT[:, gi, 1, tt + 1, :], rhs=wT[:, 512:768], start=True, stop=True)
+
+        def add_bias(k):
+            p0, p1, pc = ps_t["pl", k]
+            pb = pbpool.tile([P, 2, NG], F32, name="pb")
+            pb_t[k] = pb
+            nc.vector.tensor_tensor(out=pb[:, 0, 0:512], in0=p0[:], in1=bias_bc[:, 0:512], op=ALU.add)
+            nc.vector.tensor_tensor(out=pb[:, 1, 0:512], in0=p1[:], in1=bias_bc[:, 0:512], op=ALU.add)
+            nc.vector.tensor_tensor(
+                out=pb[:, :, 512:768], in0=pc[:].rearrange("p (t n) -> p t n", t=2),
+                in1=bias_bc[:, 512:768].unsqueeze(1).to_broadcast([P, 2, 256]), op=ALU.add,
+            )
+
+        def mx(k):
+            xc, xs = xq_t[k]
+            a0 = psum.tile([P, 512], F32, tag="A0", name="a0")
+            a1 = psum.tile([P, 512], F32, tag="A1", name="a1")
+            ac = psum.tile([P, 512], F32, tag="AC", name="ac")
+            ps_t["mx", k] = (a0, a1, ac)
+            for i in range(2):
+                dst = (a0, a1)[i]
+                for g in range(2):
+                    lo = (2 * i + g) * P
+                    nc.tensor.matmul_mx(
+                        out=dst[:], lhsT=xc[:, lo:lo + P].bitcast(FP8X4), lhsT_scale=xs[:, lo:lo + P],
+                        rhs=w_codes[:, g * NG:g * NG + 512].bitcast(FP8X4), rhs_scale=w_scales[:, g * NG:g * NG + 512],
+                        start=(g == 0), stop=(g == 1),
+                    )
+            for i in range(2):
+                for g in range(2):
+                    lo = (2 * i + g) * P
+                    nc.tensor.matmul_mx(
+                        out=ac[:, 256 * i:256 * i + 256], lhsT=xc[:, lo:lo + P].bitcast(FP8X4), lhsT_scale=xs[:, lo:lo + P],
+                        rhs=w_codes[:, g * NG + 512:g * NG + 768].bitcast(FP8X4), rhs_scale=w_scales[:, g * NG + 512:g * NG + 768],
+                        start=(g == 0), stop=(g == 1),
+                    )
+
+        def add_mx(k):
+            gi = k // 2
+            tt = 2 * (k % 2)
+            if tt == 0:
+                g4_new = gpool.tile([P, 4, NG], F32, name="g4")
+                g4_t[gi] = g4_new
+            g4 = g4_t[gi]
+            a0, a1, ac = ps_t["mx", k]
+            pb = pb_t[k]
+            nc.vector.tensor_tensor(out=g4[:, tt, 0:512], in0=a0[:], in1=pb[:, 0, 0:512], op=ALU.add)
+            nc.vector.tensor_tensor(out=g4[:, tt + 1, 0:512], in0=a1[:], in1=pb[:, 1, 0:512], op=ALU.add)
+            nc.vector.tensor_tensor(
+                out=g4[:, tt:tt + 2, 512:768], in0=ac[:].rearrange("p (t n) -> p t n", t=2),
+                in1=pb[:, :, 512:768], op=ALU.add,
+            )
+
+        def gate_functions(k):
+            g4 = g4_t[k // 2]
+            tt = 2 * (k % 2)
+            nc.scalar.activation(out=g4[:, tt:tt + 2, 0:384], in_=g4[:, tt:tt + 2, 0:384], func=ACT.Sigmoid)
+            nc.scalar.activation(out=g4[:, tt:tt + 2, 384:512], in_=g4[:, tt:tt + 2, 384:512], func=ACT.Tanh)
+            nc.scalar.activation(out=g4[:, tt:tt + 2, 512:768], in_=g4[:, tt:tt + 2, 512:768], func=ACT.Sigmoid)
+
+        def out_tiles(gi):
+            oh = opool.tile([P, 4, H], F32, name="oh")
+            oc = opool.tile([P, 4, H], F32, name="oc")
+            os_ = opool.tile([P, 2, 4, H], F32, name="os_")
+            out_t[gi] = (oh, oc, os_)
+
+        def cell_sum_gpsimd(gi):
+            g4 = g4_t[gi]
+            nc.gpsimd.tensor_tensor(out=g4[:, :, 128:256], in0=g4[:, :, 128:256], in1=c_sb[:, 4 * gi:4 * gi + 4, :], op=ALU.mult)
+            nc.gpsimd.tensor_tensor(out=g4[:, :, 384:512], in0=g4[:, :, 0:128], in1=g4[:, :, 384:512], op=ALU.mult)
+            nc.gpsimd.tensor_tensor(out=g4[:, :, 0:128], in0=g4[:, :, 128:256], in1=g4[:, :, 384:512], op=ALU.add)
+
+        def cell_scalar(t):
+            gi = t // 4
+            tt = t % 4
+            g4 = g4_t[gi]
+            oc = out_t[gi][1]
+            m = m32[:, t:t + 1]
+            nc.scalar.activation(out=g4[:, tt, 128:256], in_=g4[:, tt, 0:128], func=ACT.Tanh, scale=m)
+            nc.scalar.activation(out=oc[:, tt, :], in_=g4[:, tt, 0:128], func=ACT.Copy, scale=m)
+            if gi < NG_OUT:
+                nc.scalar.activation(out=g4[:, tt, 384:512], in_=g4[:, tt, 128:256], func=ACT.Copy, scale=m)
+
+        def outputs_gpsimd(gi):
+            g4 = g4_t[gi]
+            oh, oc, os_ = out_t[gi]
+            nc.gpsimd.tensor_tensor(out=oh[:], in0=g4[:, :, 256:384], in1=g4[:, :, 384:512], op=ALU.mult)
+            nc.gpsimd.tensor_tensor(
+                out=os_[:].rearrange("p k t c -> p t k c"),
+                in0=g4[:, :, 512:768].rearrange("p t (k c) -> p t k c", k=2),
+                in1=g4[:, :, 384:512].unsqueeze(2).to_broadcast([P, 4, 2, H]), op=ALU.mult,
+            )
+
+        def cell_vector(t):
+            gi = t // 4
+            tt = t % 4
+            g4 = g4_t[gi]
+            oc = out_t[gi][1]
+            m = m32[:, t:t + 1]
+            nc.vector.scalar_tensor_tensor(out=g4[:, tt, 128:256], in0=c_sb[:, t, :], scalar=m, in1=g4[:, tt, 128:256], op0=ALU.mult, op1=ALU.mult)
+            nc.vector.scalar_tensor_tensor(out=g4[:, tt, 384:512], in0=g4[:, tt, 384:512], scalar=m, in1=g4[:, tt, 0:128], op0=ALU.mult, op1=ALU.mult)
+            nc.vector.tensor_tensor(out=oc[:, tt, :], in0=g4[:, tt, 128:256], in1=g4[:, tt, 384:512], op=ALU.add)
+            nc.scalar.activation(out=g4[:, tt, 128:256], in_=oc[:, tt, :], func=ACT.Tanh)
+
+        def outputs_vector(t):
+            gi = t // 4
+            tt = t % 4
+            g4 = g4_t[gi]
+            oh, oc, os_ = out_t[gi]
+            m = m32[:, t:t + 1]
+            nc.vector.scalar_tensor_tensor(out=oh[:, tt, :], in0=g4[:, tt, 128:256], scalar=m, in1=g4[:, tt, 256:384], op0=ALU.mult, op1=ALU.mult)
+            nc.vector.scalar_tensor_tensor(
+                out=os_[:, :, tt, :], in0=g4[:, tt, 128:256].unsqueeze(1).to_broadcast([P, 2, H]), scalar=m,
+                in1=g4[:, tt, 512:768].rearrange("p (k c) -> p k c", k=2), op0=ALU.mult, op1=ALU.mult,
+            )
+
+        def store(gi, which, lo, n):
+            oh, oc, os_ = out_t[gi]
+            src = (oh, oc, os_[:, 0], os_[:, 1])[which]
+            nc.sync.dma_start(out=outs[which][:, 4 * gi + lo:4 * gi + lo + n, :], in_=src[:, lo:lo + n, :])
+
+        wt_ps = psum.tile([P, 6, H], BF16, tag="X0", name="wt_ps")
+        for j in range(6):
+            nc.tensor.transpose(wt_ps[:, j, :], whh_raw[:, j, :], ident_b[:])
+        nc.scalar.copy(out=wT[:], in_=wt_ps[:].rearrange("p j k -> p (j k)"))
+        hs_pe(0, "X1")
+        hs_ev(0, "S")
+        b_ps0 = psum.tile([P, 512], F32, tag="A0", name="b_ps0")
+        b_ps1 = psum.tile([P, 512], F32, tag="AC", name="b_ps1")
+        nc.tensor.matmul(out=b_ps0[:], lhsT=ones[:], rhs=braw[:, 0:512], start=True, stop=True)
+        nc.tensor.matmul(out=b_ps1[:, 0:256], lhsT=ones[:], rhs=braw[:, 512:768], start=True, stop=True)
+        nc.vector.tensor_copy(out=bias_bc[:, 0:512], in_=b_ps0[:])
+        nc.vector.tensor_copy(out=bias_bc[:, 512:768], in_=b_ps1[:, 0:256])
+        plain(0)
+        add_bias(0)
+        w_tags = ("A1", "A0", "AC", "X0", "A1", "A0")
+        for a in range(2):
+            w_pe(2 * a, w_tags[2 * a])
+            w_ev(2 * a, "S")
+            w_pe(2 * a + 1, w_tags[2 * a + 1])
+            w_ev(2 * a + 1, "V")
+            w_quant(a)
+        x_pe(0, "X1")
+        x_ev(0, "S")
+        x_pe(1, "AC")
+        x_ev(1, "V")
+        quantise(0)
+        w_pe(4, w_tags[4])
+        w_ev(4, "S")
+        w_pe(5, w_tags[5])
+        w_ev(5, "V")
+        w_quant(2)
+        hs_pe(1, "X0")
+        hs_ev(1, "S")
+        x_pe(2, "X1")
+        x_ev(2, "S")
+        x_pe(3, "X0")
+        x_ev(3, "S")
+        mx(0)
+        plain(1)
+        nc.vector.tensor_copy(out=m32[:], in_=m_bf[:])
+        quantise(1)
+        x_pe(4, "X1")
+        x_ev(4, "S")
+        x_pe(5, "X0")
+        x_ev(5, "S")
+
+        def group_at(j, off, limit):
+            if (j - off) % 2 == 0 and 0 <= (j - off) // 2 < limit:
+                return (j - off) // 2
+            return -1
+
+        for j in range(NPAIR + 8):
+            kk = j + LA + 2
+            do_hs = kk % 2 == 0 and 2 <= kk // 2 < NGROUP
+            if do_hs:
+                hs_pe(kk // 2, "X1")
+            if j + 1 < NPAIR:
+                mx(j + 1)
+            if j < NPAIR:
+                add_mx(j)
+            if j + QL < NPAIR:
+                quantise(j + QL)
+            if 0 <= j - 1 < NPAIR:
+                gate_functions(j - 1)
+            if do_hs:
+                hs_ev(kk // 2, "S")
+            g = group_at(j, 3, NG_SUM)
+            if g >= 0:
+                out_tiles(g)
+                cell_sum_gpsimd(g)
+            g = group_at(j, 4, NG_SUM)
+            if g >= 0:
+                cell_scalar(4 * g)
+                cell_scalar(4 * g + 1)
+            g = group_at(j, 5, NG_SUM)
+            if g >= 0:
+                cell_scalar(4 * g + 2)
+                cell_scalar(4 * g + 3)
+                store(g, 1, 0, 4)
+            g = group_at(j, 6, NG_OUT)
+            if g >= 0:
+                outputs_gpsimd(g)
+                store(g, 0, 0, 4)
+                store(g, 2, 0, 4)
+                store(g, 3, 0, 4)
+            if j + XL < NPAIR:
+                if j + XL + 5 < NPAIR:
+                    load_x(j + XL + 5)
+                x_pe(2 * (j + XL), "X0")
+                x_pe(2 * (j + XL) + 1, "X1")
+                x_ev(2 * (j + XL), "S")
+                x_ev(2 * (j + XL) + 1, "S")
+            if j + LA + 1 < NPAIR:
+                plain(j + LA + 1)
+            if j + LA < NPAIR:
+                add_bias(j + LA)
+            g = group_at(j, 6, NG_SUM)
+            if g >= NG_OUT:
+                for tt in range(4):
+                    outputs_vector(4 * g + tt)
+                store(g, 0, 0, 4)
+                store(g, 2, 0, 4)
+                store(g, 3, 0, 4)
+            k1 = j - 1
+            k2 = j - 2
+            if 0 <= k1 < NPAIR and k1 // 2 >= NG_SUM:
+                if k1 % 2 == 0:
+                    out_tiles(k1 // 2)
+                cell_vector(2 * k1)
+                cell_vector(2 * k1 + 1)
+            if 0 <= k2 < NPAIR and k2 // 2 >= NG_SUM:
+                outputs_vector(2 * k2)
+                outputs_vector(2 * k2 + 1)
+                for which in (1, 0, 2, 3):
+                    store(k2 // 2, which, 2 * (k2 % 2), 2)

@@ -18,13 +18,8 @@ H = 128
 NG = 768
 NT = B // P
 NPAIR = NT // 2
-NGROUP = NT // 4
-LA = 1
-XL = 3
-QL = 2
-PINNED = True
 NG_SUM = 7
-NG_OUT = 5
+NG_OUT = 6
 
 FLOPS = 2 * B * (D_IN * NG + H * 512 + H * 256)
 BYTES = 2 * (B * D_IN + 3 * B * H + B + NG * D_IN + 768 * H + 2 * NG) + 4 * 4 * B * H
@@ -37,14 +32,15 @@ def tile_share_lstm_cell_t_kernel(
     nc = tc.nc
     with ExitStack() as ctx:
         const = ctx.enter_context(tc.tile_pool(name="const", bufs=1))
-        xpool = ctx.enter_context(tc.tile_pool(name="xpool", bufs=8))
-        qpool = ctx.enter_context(tc.tile_pool(name="qpool", bufs=3))
-        pbpool = ctx.enter_context(tc.tile_pool(name="pbpool", bufs=LA + 1))
+        xpool = ctx.enter_context(tc.tile_pool(name="xpool", bufs=14))
+        gxpool = ctx.enter_context(tc.tile_pool(name="gxpool", bufs=4))
+        qpool = ctx.enter_context(tc.tile_pool(name="qpool", bufs=4))
+        hspool = ctx.enter_context(tc.tile_pool(name="hspool", bufs=4))
+        pbpool = ctx.enter_context(tc.tile_pool(name="pbpool", bufs=3))
         gpool = ctx.enter_context(tc.tile_pool(name="gpool", bufs=5))
         opool = ctx.enter_context(tc.tile_pool(name="opool", bufs=3))
         psum = ctx.enter_context(tc.psum_pool(name="psum", bufs=1))
-        if PINNED:
-            ctx.enter_context(tc.manual_schedule())
+        ctx.enter_context(tc.manual_schedule())
 
         xv = x_in.rearrange("(p t) k -> p t k", t=NT)
         hv = h_minors.rearrange("(p t) k -> p t k", t=NT)
@@ -57,24 +53,25 @@ def tile_share_lstm_cell_t_kernel(
         braw = const.tile([P, NG], BF16)
         m_bf = const.tile([P, NT], BF16)
         m32 = const.tile([P, NT], F32)
-        w_raw = const.tile([P, 6, D_IN], BF16)
         h_sb = const.tile([P, NT, H], BF16)
         s_sb = const.tile([P, NT, H], BF16)
         c_sb = const.tile([P, NT, H], BF16)
         ident_f = const.tile([P, P], F32)
         ident_b = const.tile([P, P], BF16)
         ones = const.tile([P, P], BF16)
+        warm = const.tile([P, 8], F32)
         wT = const.tile([P, NG], BF16)
         bias_bc = const.tile([P, NG], F32)
-        hsT = const.tile([P, NGROUP, 2, 4, H], BF16)
-        w_grp = const.tile([P, 2, NG, 2], F32, align_bytes=64)
         w_codes = const.tile([P, 2 * NG], U32, align_bytes=64)
         w_scales = const.tile([P, 2 * NG], U8, align_bytes=64)
 
+        w_raw_t = {}
+        w_grp_t = {}
         xp_t = {}
         ps_t = {}
         xg_t = {}
         xq_t = {}
+        hsT_t = {}
         pb_t = {}
         g4_t = {}
         out_t = {}
@@ -84,64 +81,54 @@ def tile_share_lstm_cell_t_kernel(
             nc.sync.dma_start(out=x_sb[:], in_=xv[:, 2 * k:2 * k + 2, :])
             xp_t[k] = x_sb
 
+        def load_w(a):
+            w_sb = xpool.tile([P, 2, D_IN], BF16, name="x_sb")
+            nc.sync.dma_start(out=w_sb[:], in_=wv[:, 2 * a:2 * a + 2, :])
+            w_raw_t[a] = w_sb
+
+        def load_hs(lo, n):
+            nc.sync.dma_start(out=h_sb[:, lo:lo + n, :], in_=hv[:, lo:lo + n, :])
+            nc.sync.dma_start(out=s_sb[:, lo:lo + n, :], in_=sv[:, lo:lo + n, :])
+
         def copy_out(eng, out, in_):
             if eng == "V":
                 nc.vector.tensor_copy(out=out, in_=in_)
             else:
                 nc.scalar.copy(out=out, in_=in_)
 
-        nc.vector.memset(braw[:], 0.0)
-        nc.vector.memset(ones[:], 1.0)
-        make_identity(nc, ident_b[:])
-        make_identity(nc, ident_f[:])
-        nc.scalar.dma_start(out=braw[0:1, :], in_=bias_ih.unsqueeze(0))
-        nc.scalar.dma_start(out=braw[1:2, 0:512], in_=bias_hh.unsqueeze(0))
-        nc.scalar.dma_start(out=braw[1:2, 512:768], in_=bias_sh.unsqueeze(0))
-        nc.sync.dma_start(out=whh_raw[:, 0:4, :], in_=weight_hh.rearrange("(j p) k -> p j k", p=P))
-        nc.sync.dma_start(out=whh_raw[:, 4:6, :], in_=weight_sh.rearrange("(j p) k -> p j k", p=P))
-        nc.sync.dma_start(out=h_sb[:, 0:8, :], in_=hv[:, 0:8, :])
-        nc.sync.dma_start(out=s_sb[:, 0:8, :], in_=sv[:, 0:8, :])
-        nc.sync.dma_start(out=w_raw[:, 0:2, :], in_=wv[:, 0:2, :])
-        nc.sync.dma_start(out=w_raw[:, 2:4, :], in_=wv[:, 2:4, :])
-        load_x(0)
-        nc.sync.dma_start(out=w_raw[:, 4:6, :], in_=wv[:, 4:6, :])
-        load_x(1)
-        nc.scalar.dma_start(out=m_bf[:], in_=mask.rearrange("(p t) -> p t", t=NT))
-        load_x(2)
-        nc.sync.dma_start(out=h_sb[:, 8:NT, :], in_=hv[:, 8:NT, :])
-        nc.sync.dma_start(out=s_sb[:, 8:NT, :], in_=sv[:, 8:NT, :])
-        load_x(3)
-        nc.sync.dma_start(out=c_sb[:], in_=cv)
-        for k in range(4, 8):
-            load_x(k)
+        def hs_pe(k, tag):
+            hs_ps = psum.tile([P, 2, 2, H], BF16, tag=tag, name="hs_ps")
+            ps_t["hs", k] = hs_ps
+            for tt in range(2):
+                nc.tensor.transpose(hs_ps[:, 0, tt, :], h_sb[:, 2 * k + tt, :], ident_b[:])
+            for tt in range(2):
+                nc.tensor.transpose(hs_ps[:, 1, tt, :], s_sb[:, 2 * k + tt, :], ident_b[:])
 
-        def hs_pe(gi, tag):
-            hs_ps = psum.tile([P, 2, 4, H], BF16, tag=tag, name="hs_ps")
-            ps_t["hs", gi] = hs_ps
-            for tt in range(4):
-                nc.tensor.transpose(hs_ps[:, 0, tt, :], h_sb[:, 4 * gi + tt, :], ident_b[:])
-            for tt in range(4):
-                nc.tensor.transpose(hs_ps[:, 1, tt, :], s_sb[:, 4 * gi + tt, :], ident_b[:])
-
-        def hs_ev(gi, eng):
-            copy_out(eng, hsT[:, gi], ps_t["hs", gi][:])
+        def hs_ev(k, eng):
+            hsT = hspool.tile([P, 2, 2, H], BF16, name="hsT")
+            hsT_t[k] = hsT
+            copy_out(eng, hsT[:], ps_t["hs", k][:])
 
         def w_pe(j, tag):
             w_ps = psum.tile([P, 4, P], F32, tag=tag, name="w_ps")
             ps_t["w", j] = w_ps
-            ww = w_raw[:, j, :].bitcast(F32)
+            ww = w_raw_t[j // 2][:, j % 2, :].bitcast(F32)
             for q in range(4):
                 nc.tensor.transpose(w_ps[:, q, :], ww[:, 256 * (q // 2) + q % 2:256 * (q // 2) + 256:2], ident_f[:])
 
         def w_ev(j, eng):
-            copy_out(eng, w_grp[:, :, P * j:P * j + P, :], ps_t["w", j][:].rearrange("p (g u) r -> p g r u", g=2))
+            if j % 2 == 0:
+                w_grp = gxpool.tile([P, 2, 2 * P, 2], F32, align_bytes=64, name="xg")
+                w_grp_t[j // 2] = w_grp
+            lo = P * (j % 2)
+            copy_out(eng, w_grp_t[j // 2][:, :, lo:lo + P, :], ps_t["w", j][:].rearrange("p (g u) r -> p g r u", g=2))
 
         def w_quant(a):
             for g in range(2):
                 lo = g * NG + 256 * a
                 nc.vector.quantize_mx(
                     out=w_codes[:, lo:lo + 256].bitcast(FP8X4), scales=w_scales[:, lo:lo + 256],
-                    in_=w_grp[:, g, 256 * a:256 * a + 256, :].rearrange("p n u -> p (n u)").bitcast(BF16),
+                    in_=w_grp_t[a][:, g].rearrange("p n u -> p (n u)").bitcast(BF16),
                 )
 
         def x_pe(t, tag):
@@ -154,7 +141,7 @@ def tile_share_lstm_cell_t_kernel(
         def x_ev(t, eng):
             k = t // 2
             if t % 2 == 0:
-                xg_new = qpool.tile([P, 2, 2, P, 2], F32, align_bytes=64, name="xg")
+                xg_new = gxpool.tile([P, 2, 2, P, 2], F32, align_bytes=64, name="xg")
                 xg_t[k] = xg_new
             copy_out(eng, xg_t[k][:, t % 2], ps_t["x", t][:].rearrange("p (g u) r -> p g r u", g=2))
 
@@ -167,26 +154,24 @@ def tile_share_lstm_cell_t_kernel(
                 in_=xg_t[k][:].rearrange("p t g r u -> p (t g r u)").bitcast(BF16),
             )
 
-        def plain(k):
-            gi = k // 2
-            tt = 2 * (k % 2)
-            p0 = psum.tile([P, 512], F32, tag="P0", name="p0")
-            p1 = psum.tile([P, 512], F32, tag="P1", name="p1")
+        def plain_main(k, i):
+            p_ps = psum.tile([P, 512], F32, tag="P%d" % i, name="p_ps")
+            ps_t["p", k, i] = p_ps
+            nc.tensor.matmul(out=p_ps[:], lhsT=hsT_t[k][:, 0, i, :], rhs=wT[:, 0:512], start=True, stop=True)
+
+        def plain_share(k):
             pc = psum.tile([P, 512], F32, tag="PC", name="pc")
-            ps_t["pl", k] = (p0, p1, pc)
-            nc.tensor.matmul(out=p0[:], lhsT=hsT[:, gi, 0, tt, :], rhs=wT[:, 0:512], start=True, stop=True)
-            nc.tensor.matmul(out=p1[:], lhsT=hsT[:, gi, 0, tt + 1, :], rhs=wT[:, 0:512], start=True, stop=True)
-            nc.tensor.matmul(out=pc[:, 0:256], lhsT=hsT[:, gi, 1, tt, :], rhs=wT[:, 512:768], start=True, stop=True)
-            nc.tensor.matmul(out=pc[:, 256:512], lhsT=hsT[:, gi, 1, tt + 1, :], rhs=wT[:, 512:768], start=True, stop=True)
+            ps_t["pc", k] = pc
+            for i in range(2):
+                nc.tensor.matmul(out=pc[:, 256 * i:256 * i + 256], lhsT=hsT_t[k][:, 1, i, :], rhs=wT[:, 512:768], start=True, stop=True)
 
         def add_bias(k):
-            p0, p1, pc = ps_t["pl", k]
             pb = pbpool.tile([P, 2, NG], F32, name="pb")
             pb_t[k] = pb
-            nc.vector.tensor_tensor(out=pb[:, 0, 0:512], in0=p0[:], in1=bias_bc[:, 0:512], op=ALU.add)
-            nc.vector.tensor_tensor(out=pb[:, 1, 0:512], in0=p1[:], in1=bias_bc[:, 0:512], op=ALU.add)
+            for i in range(2):
+                nc.vector.tensor_tensor(out=pb[:, i, 0:512], in0=ps_t["p", k, i][:], in1=bias_bc[:, 0:512], op=ALU.add)
             nc.vector.tensor_tensor(
-                out=pb[:, :, 512:768], in0=pc[:].rearrange("p (t n) -> p t n", t=2),
+                out=pb[:, :, 512:768], in0=ps_t["pc", k][:].rearrange("p (t n) -> p t n", t=2),
                 in1=bias_bc[:, 512:768].unsqueeze(1).to_broadcast([P, 2, 256]), op=ALU.add,
             )
 
@@ -230,12 +215,12 @@ def tile_share_lstm_cell_t_kernel(
                 in1=pb[:, :, 512:768], op=ALU.add,
             )
 
-        def gate_functions(k):
-            g4 = g4_t[k // 2]
-            tt = 2 * (k % 2)
-            nc.scalar.activation(out=g4[:, tt:tt + 2, 0:384], in_=g4[:, tt:tt + 2, 0:384], func=ACT.Sigmoid)
-            nc.scalar.activation(out=g4[:, tt:tt + 2, 384:512], in_=g4[:, tt:tt + 2, 384:512], func=ACT.Tanh)
-            nc.scalar.activation(out=g4[:, tt:tt + 2, 512:768], in_=g4[:, tt:tt + 2, 512:768], func=ACT.Sigmoid)
+        def gate_functions(t, n):
+            g4 = g4_t[t // 4]
+            tt = t % 4
+            nc.scalar.activation(out=g4[:, tt:tt + n, 0:384], in_=g4[:, tt:tt + n, 0:384], func=ACT.Sigmoid)
+            nc.scalar.activation(out=g4[:, tt:tt + n, 384:512], in_=g4[:, tt:tt + n, 384:512], func=ACT.Tanh)
+            nc.scalar.activation(out=g4[:, tt:tt + n, 512:768], in_=g4[:, tt:tt + n, 512:768], func=ACT.Sigmoid)
 
         def out_tiles(gi):
             oh = opool.tile([P, 4, H], F32, name="oh")
@@ -243,11 +228,11 @@ def tile_share_lstm_cell_t_kernel(
             os_ = opool.tile([P, 2, 4, H], F32, name="os_")
             out_t[gi] = (oh, oc, os_)
 
-        def cell_sum_gpsimd(gi):
+        def cell_sum_gpsimd(gi, lo, n):
             g4 = g4_t[gi]
-            nc.gpsimd.tensor_tensor(out=g4[:, :, 128:256], in0=g4[:, :, 128:256], in1=c_sb[:, 4 * gi:4 * gi + 4, :], op=ALU.mult)
-            nc.gpsimd.tensor_tensor(out=g4[:, :, 384:512], in0=g4[:, :, 0:128], in1=g4[:, :, 384:512], op=ALU.mult)
-            nc.gpsimd.tensor_tensor(out=g4[:, :, 0:128], in0=g4[:, :, 128:256], in1=g4[:, :, 384:512], op=ALU.add)
+            nc.gpsimd.tensor_tensor(out=g4[:, lo:lo + n, 128:256], in0=g4[:, lo:lo + n, 128:256], in1=c_sb[:, 4 * gi + lo:4 * gi + lo + n, :], op=ALU.mult)
+            nc.gpsimd.tensor_tensor(out=g4[:, lo:lo + n, 384:512], in0=g4[:, lo:lo + n, 0:128], in1=g4[:, lo:lo + n, 384:512], op=ALU.mult)
+            nc.gpsimd.tensor_tensor(out=g4[:, lo:lo + n, 0:128], in0=g4[:, lo:lo + n, 128:256], in1=g4[:, lo:lo + n, 384:512], op=ALU.add)
 
         def cell_scalar(t):
             gi = t // 4
@@ -279,7 +264,11 @@ def tile_share_lstm_cell_t_kernel(
             nc.vector.scalar_tensor_tensor(out=g4[:, tt, 128:256], in0=c_sb[:, t, :], scalar=m, in1=g4[:, tt, 128:256], op0=ALU.mult, op1=ALU.mult)
             nc.vector.scalar_tensor_tensor(out=g4[:, tt, 384:512], in0=g4[:, tt, 384:512], scalar=m, in1=g4[:, tt, 0:128], op0=ALU.mult, op1=ALU.mult)
             nc.vector.tensor_tensor(out=oc[:, tt, :], in0=g4[:, tt, 128:256], in1=g4[:, tt, 384:512], op=ALU.add)
-            nc.scalar.activation(out=g4[:, tt, 128:256], in_=oc[:, tt, :], func=ACT.Tanh)
+
+        def cell_tanh(t):
+            gi = t // 4
+            tt = t % 4
+            nc.scalar.activation(out=g4_t[gi][:, tt, 128:256], in_=out_t[gi][1][:, tt, :], func=ACT.Tanh)
 
         def outputs_vector(t):
             gi = t // 4
@@ -298,118 +287,166 @@ def tile_share_lstm_cell_t_kernel(
             src = (oh, oc, os_[:, 0], os_[:, 1])[which]
             nc.sync.dma_start(out=outs[which][:, 4 * gi + lo:4 * gi + lo + n, :], in_=src[:, lo:lo + n, :])
 
+
+        nc.vector.memset(ones[:], 1.0)
+        nc.vector.memset(braw[:], 0.0)
+        nc.scalar.activation(out=warm[:], in_=ones[:, 0:8], func=ACT.Sigmoid)
+        make_identity(nc, ident_f[:])
+        make_identity(nc, ident_b[:])
+        nc.scalar.dma_start(out=braw[0:1, :], in_=bias_ih.unsqueeze(0))
+        nc.scalar.dma_start(out=braw[1:2, 0:512], in_=bias_hh.unsqueeze(0))
+        nc.scalar.dma_start(out=braw[1:2, 512:768], in_=bias_sh.unsqueeze(0))
+        nc.scalar.dma_start(out=m_bf[:], in_=mask.rearrange("(p t) -> p t", t=NT))
+        load_w(0)
+        nc.sync.dma_start(out=whh_raw[:, 0:4, :], in_=weight_hh.rearrange("(j p) k -> p j k", p=P))
+        nc.sync.dma_start(out=whh_raw[:, 4:6, :], in_=weight_sh.rearrange("(j p) k -> p j k", p=P))
+        load_hs(0, 4)
+        load_w(1)
+        load_w(2)
+        load_x(0)
+        load_x(1)
+        load_hs(4, 12)
+        load_x(2)
+        load_x(3)
+        nc.sync.dma_start(out=c_sb[:], in_=cv)
+        load_x(4)
+        load_hs(16, 16)
+        for k in range(5, NPAIR):
+            load_x(k)
+
+        w_pe(0, "AC")
+        w_ev(0, "V")
+        w_pe(1, "A0")
+        w_ev(1, "V")
+        w_quant(0)
         wt_ps = psum.tile([P, 6, H], BF16, tag="X0", name="wt_ps")
         for j in range(6):
             nc.tensor.transpose(wt_ps[:, j, :], whh_raw[:, j, :], ident_b[:])
         nc.scalar.copy(out=wT[:], in_=wt_ps[:].rearrange("p j k -> p (j k)"))
         hs_pe(0, "X1")
         hs_ev(0, "S")
-        b_ps0 = psum.tile([P, 512], F32, tag="A0", name="b_ps0")
-        b_ps1 = psum.tile([P, 512], F32, tag="AC", name="b_ps1")
+        b_ps0 = psum.tile([P, 512], F32, tag="A1", name="b_ps0")
         nc.tensor.matmul(out=b_ps0[:], lhsT=ones[:], rhs=braw[:, 0:512], start=True, stop=True)
+        nc.scalar.copy(out=bias_bc[:, 0:512], in_=b_ps0[:])
+        b_ps1 = psum.tile([P, 512], F32, tag="X0", name="b_ps1")
         nc.tensor.matmul(out=b_ps1[:, 0:256], lhsT=ones[:], rhs=braw[:, 512:768], start=True, stop=True)
-        nc.vector.tensor_copy(out=bias_bc[:, 0:512], in_=b_ps0[:])
-        nc.vector.tensor_copy(out=bias_bc[:, 512:768], in_=b_ps1[:, 0:256])
-        plain(0)
+        nc.scalar.copy(out=bias_bc[:, 512:768], in_=b_ps1[:, 0:256])
+        plain_main(0, 0)
+        plain_main(0, 1)
+        plain_share(0)
+        hs_pe(1, "X1")
+        hs_ev(1, "S")
+        w_pe(2, "AC")
+        w_ev(2, "V")
+        w_pe(3, "A0")
+        w_ev(3, "V")
+        w_quant(1)
         add_bias(0)
-        w_tags = ("A1", "A0", "AC", "X0", "A1", "A0")
-        for a in range(2):
-            w_pe(2 * a, w_tags[2 * a])
-            w_ev(2 * a, "S")
-            w_pe(2 * a + 1, w_tags[2 * a + 1])
-            w_ev(2 * a + 1, "V")
-            w_quant(a)
+        w_pe(4, "A1")
+        w_ev(4, "S")
+        w_pe(5, "X0")
+        w_ev(5, "S")
+        w_quant(2)
         x_pe(0, "X1")
         x_ev(0, "S")
         x_pe(1, "AC")
-        x_ev(1, "V")
+        x_ev(1, "S")
         quantise(0)
-        w_pe(4, w_tags[4])
-        w_ev(4, "S")
-        w_pe(5, w_tags[5])
-        w_ev(5, "V")
-        w_quant(2)
-        hs_pe(1, "X0")
-        hs_ev(1, "S")
-        x_pe(2, "X1")
+        plain_main(1, 0)
+        plain_main(1, 1)
+        plain_share(1)
+        hs_pe(2, "A1")
+        hs_ev(2, "S")
+        x_pe(2, "X0")
         x_ev(2, "S")
-        x_pe(3, "X0")
+        x_pe(3, "X1")
         x_ev(3, "S")
         mx(0)
-        plain(1)
-        nc.vector.tensor_copy(out=m32[:], in_=m_bf[:])
-        quantise(1)
-        x_pe(4, "X1")
-        x_ev(4, "S")
-        x_pe(5, "X0")
-        x_ev(5, "S")
+        nc.gpsimd.tensor_copy(out=m32[:], in_=m_bf[:])
 
         def group_at(j, off, limit):
             if (j - off) % 2 == 0 and 0 <= (j - off) // 2 < limit:
                 return (j - off) // 2
             return -1
 
-        for j in range(NPAIR + 8):
-            kk = j + LA + 2
-            do_hs = kk % 2 == 0 and 2 <= kk // 2 < NGROUP
-            if do_hs:
-                hs_pe(kk // 2, "X1")
+        bank = 0
+        for j in range(NPAIR):
+            if j + 1 < NPAIR:
+                if j > 0:
+                    quantise(j + 1)
+                add_bias(j + 1)
+                if j == 0:
+                    quantise(j + 1)
+            if 0 <= j - 1:
+                gate_functions(2 * (j - 1), 2)
+            if j + 2 < NPAIR:
+                k = j + 2
+                plain_main(k, 0)
+                x_pe(2 * k, "X%d" % (bank % 2))
+                plain_main(k, 1)
+                x_pe(2 * k + 1, "X%d" % ((bank + 1) % 2))
+                plain_share(k)
+                bank = bank + 2
+                x_ev(2 * k, "S")
+                x_ev(2 * k + 1, "S")
+            if j + 3 < NPAIR:
+                hs_pe(j + 3, "X%d" % (bank % 2))
+                bank = bank + 1
+                hs_ev(j + 3, "S")
+            if j == NPAIR - 1:
+                outputs_vector(2 * j - 6)
+                outputs_vector(2 * j - 5)
+            add_mx(j)
             if j + 1 < NPAIR:
                 mx(j + 1)
-            if j < NPAIR:
-                add_mx(j)
-            if j + QL < NPAIR:
-                quantise(j + QL)
-            if 0 <= j - 1 < NPAIR:
-                gate_functions(j - 1)
-            if do_hs:
-                hs_ev(kk // 2, "S")
-            g = group_at(j, 3, NG_SUM)
+            g = group_at(j, 2, NG_OUT)
             if g >= 0:
                 out_tiles(g)
-                cell_sum_gpsimd(g)
-            g = group_at(j, 4, NG_SUM)
+                cell_sum_gpsimd(g, 0, 4)
+            g = group_at(j, 3, NG_OUT)
             if g >= 0:
                 cell_scalar(4 * g)
                 cell_scalar(4 * g + 1)
-            g = group_at(j, 5, NG_SUM)
+            g = group_at(j, 4, NG_OUT)
             if g >= 0:
                 cell_scalar(4 * g + 2)
                 cell_scalar(4 * g + 3)
                 store(g, 1, 0, 4)
-            g = group_at(j, 6, NG_OUT)
+            g = group_at(j, 5, NG_OUT)
             if g >= 0:
                 outputs_gpsimd(g)
                 store(g, 0, 0, 4)
                 store(g, 2, 0, 4)
                 store(g, 3, 0, 4)
-            if j + XL < NPAIR:
-                if j + XL + 5 < NPAIR:
-                    load_x(j + XL + 5)
-                x_pe(2 * (j + XL), "X0")
-                x_pe(2 * (j + XL) + 1, "X1")
-                x_ev(2 * (j + XL), "S")
-                x_ev(2 * (j + XL) + 1, "S")
-            if j + LA + 1 < NPAIR:
-                plain(j + LA + 1)
-            if j + LA < NPAIR:
-                add_bias(j + LA)
-            g = group_at(j, 6, NG_SUM)
-            if g >= NG_OUT:
-                for tt in range(4):
-                    outputs_vector(4 * g + tt)
-                store(g, 0, 0, 4)
-                store(g, 2, 0, 4)
-                store(g, 3, 0, 4)
-            k1 = j - 1
-            k2 = j - 2
-            if 0 <= k1 < NPAIR and k1 // 2 >= NG_SUM:
-                if k1 % 2 == 0:
-                    out_tiles(k1 // 2)
-                cell_vector(2 * k1)
-                cell_vector(2 * k1 + 1)
-            if 0 <= k2 < NPAIR and k2 // 2 >= NG_SUM:
-                outputs_vector(2 * k2)
-                outputs_vector(2 * k2 + 1)
-                for which in (1, 0, 2, 3):
-                    store(k2 // 2, which, 2 * (k2 % 2), 2)
+            if NG_OUT <= (j - 1) // 2 < NG_SUM:
+                if j % 2 == 1:
+                    out_tiles((j - 1) // 2)
+                cell_sum_gpsimd((j - 1) // 2, 2 * ((j - 1) % 2), 2)
+            if NG_OUT <= (j - 2) // 2 < NG_SUM:
+                cell_scalar(2 * (j - 2))
+                cell_scalar(2 * (j - 2) + 1)
+        g = NG_SUM
+        store(g - 1, 1, 0, 4)
+        out_tiles(g)
+        cell_vector(4 * g)
+        cell_vector(4 * g + 1)
+        gate_functions(4 * g + 2, 1)
+        cell_tanh(4 * g)
+        cell_tanh(4 * g + 1)
+        gate_functions(4 * g + 3, 1)
+        cell_vector(4 * g + 2)
+        cell_tanh(4 * g + 2)
+        outputs_vector(4 * g - 2)
+        outputs_vector(4 * g - 1)
+        for which in (0, 2, 3):
+            store(g - 1, which, 0, 4)
+        outputs_vector(4 * g)
+        outputs_vector(4 * g + 1)
+        for which in (1, 0, 2, 3):
+            store(g, which, 0, 2)
+        cell_vector(4 * g + 3)
+        cell_tanh(4 * g + 3)
+        outputs_vector(4 * g + 2)
+        outputs_vector(4 * g + 3)
+        for which in (1, 0, 2, 3):
+            store(g, which, 2, 2)

@@ -18,8 +18,10 @@ H = 128
 NG = 768
 NT = B // P
 NPAIR = NT // 2
-NG_SUM = 7
-NG_OUT = 6
+G_TILES = 28
+G_FIRST = 8
+G_PAIRED = 20
+V_OUT = 24
 
 FLOPS = 2 * B * (D_IN * NG + H * 512 + H * 256)
 BYTES = 2 * (B * D_IN + 3 * B * H + B + NG * D_IN + 768 * H + 2 * NG) + 4 * 4 * B * H
@@ -81,10 +83,11 @@ def tile_share_lstm_cell_t_kernel(
             nc.sync.dma_start(out=x_sb[:], in_=xv[:, 2 * k:2 * k + 2, :])
             xp_t[k] = x_sb
 
-        def load_w(a):
-            w_sb = xpool.tile([P, 2, D_IN], BF16, name="x_sb")
-            nc.sync.dma_start(out=w_sb[:], in_=wv[:, 2 * a:2 * a + 2, :])
-            w_raw_t[a] = w_sb
+        def load_w(a, j):
+            if j == 0:
+                w_sb = xpool.tile([P, 2, D_IN], BF16, name="x_sb")
+                w_raw_t[a] = w_sb
+            nc.sync.dma_start(out=w_raw_t[a][:, j, :], in_=wv[:, 2 * a + j, :])
 
         def load_hs(lo, n):
             nc.sync.dma_start(out=h_sb[:, lo:lo + n, :], in_=hv[:, lo:lo + n, :])
@@ -181,15 +184,7 @@ def tile_share_lstm_cell_t_kernel(
             a1 = psum.tile([P, 512], F32, tag="A1", name="a1")
             ac = psum.tile([P, 512], F32, tag="AC", name="ac")
             ps_t["mx", k] = (a0, a1, ac)
-            for i in range(2):
-                dst = (a0, a1)[i]
-                for g in range(2):
-                    lo = (2 * i + g) * P
-                    nc.tensor.matmul_mx(
-                        out=dst[:], lhsT=xc[:, lo:lo + P].bitcast(FP8X4), lhsT_scale=xs[:, lo:lo + P],
-                        rhs=w_codes[:, g * NG:g * NG + 512].bitcast(FP8X4), rhs_scale=w_scales[:, g * NG:g * NG + 512],
-                        start=(g == 0), stop=(g == 1),
-                    )
+            mx_main(k, 0, a0)
             for i in range(2):
                 for g in range(2):
                     lo = (2 * i + g) * P
@@ -198,6 +193,17 @@ def tile_share_lstm_cell_t_kernel(
                         rhs=w_codes[:, g * NG + 512:g * NG + 768].bitcast(FP8X4), rhs_scale=w_scales[:, g * NG + 512:g * NG + 768],
                         start=(g == 0), stop=(g == 1),
                     )
+            mx_main(k, 1, a1)
+
+        def mx_main(k, i, dst):
+            xc, xs = xq_t[k]
+            for g in range(2):
+                lo = (2 * i + g) * P
+                nc.tensor.matmul_mx(
+                    out=dst[:], lhsT=xc[:, lo:lo + P].bitcast(FP8X4), lhsT_scale=xs[:, lo:lo + P],
+                    rhs=w_codes[:, g * NG:g * NG + 512].bitcast(FP8X4), rhs_scale=w_scales[:, g * NG:g * NG + 512],
+                    start=(g == 0), stop=(g == 1),
+                )
 
         def add_mx(k):
             gi = k // 2
@@ -209,11 +215,11 @@ def tile_share_lstm_cell_t_kernel(
             a0, a1, ac = ps_t["mx", k]
             pb = pb_t[k]
             nc.vector.tensor_tensor(out=g4[:, tt, 0:512], in0=a0[:], in1=pb[:, 0, 0:512], op=ALU.add)
-            nc.vector.tensor_tensor(out=g4[:, tt + 1, 0:512], in0=a1[:], in1=pb[:, 1, 0:512], op=ALU.add)
             nc.vector.tensor_tensor(
                 out=g4[:, tt:tt + 2, 512:768], in0=ac[:].rearrange("p (t n) -> p t n", t=2),
                 in1=pb[:, :, 512:768], op=ALU.add,
             )
+            nc.vector.tensor_tensor(out=g4[:, tt + 1, 0:512], in0=a1[:], in1=pb[:, 1, 0:512], op=ALU.add)
 
         def gate_functions(t, n):
             g4 = g4_t[t // 4]
@@ -242,17 +248,17 @@ def tile_share_lstm_cell_t_kernel(
             m = m32[:, t:t + 1]
             nc.scalar.activation(out=g4[:, tt, 128:256], in_=g4[:, tt, 0:128], func=ACT.Tanh, scale=m)
             nc.scalar.activation(out=oc[:, tt, :], in_=g4[:, tt, 0:128], func=ACT.Copy, scale=m)
-            if gi < NG_OUT:
+            if t < V_OUT or t >= V_OUT + 2:
                 nc.scalar.activation(out=g4[:, tt, 384:512], in_=g4[:, tt, 128:256], func=ACT.Copy, scale=m)
 
-        def outputs_gpsimd(gi):
+        def outputs_gpsimd(gi, lo, n):
             g4 = g4_t[gi]
             oh, oc, os_ = out_t[gi]
-            nc.gpsimd.tensor_tensor(out=oh[:], in0=g4[:, :, 256:384], in1=g4[:, :, 384:512], op=ALU.mult)
+            nc.gpsimd.tensor_tensor(out=oh[:, lo:lo + n, :], in0=g4[:, lo:lo + n, 256:384], in1=g4[:, lo:lo + n, 384:512], op=ALU.mult)
             nc.gpsimd.tensor_tensor(
-                out=os_[:].rearrange("p k t c -> p t k c"),
-                in0=g4[:, :, 512:768].rearrange("p t (k c) -> p t k c", k=2),
-                in1=g4[:, :, 384:512].unsqueeze(2).to_broadcast([P, 4, 2, H]), op=ALU.mult,
+                out=os_[:, :, lo:lo + n, :].rearrange("p k t c -> p t k c"),
+                in0=g4[:, lo:lo + n, 512:768].rearrange("p t (k c) -> p t k c", k=2),
+                in1=g4[:, lo:lo + n, 384:512].unsqueeze(2).to_broadcast([P, n, 2, H]), op=ALU.mult,
             )
 
         def cell_vector(t):
@@ -282,10 +288,12 @@ def tile_share_lstm_cell_t_kernel(
                 in1=g4[:, tt, 512:768].rearrange("p (k c) -> p k c", k=2), op0=ALU.mult, op1=ALU.mult,
             )
 
-        def store(gi, which, lo, n):
+        def store(t, n, which, eng):
+            gi = t // 4
+            lo = t % 4
             oh, oc, os_ = out_t[gi]
             src = (oh, oc, os_[:, 0], os_[:, 1])[which]
-            nc.sync.dma_start(out=outs[which][:, 4 * gi + lo:4 * gi + lo + n, :], in_=src[:, lo:lo + n, :])
+            eng.dma_start(out=outs[which][:, t:t + n, :], in_=src[:, lo:lo + n, :])
 
 
         nc.vector.memset(ones[:], 1.0)
@@ -297,12 +305,15 @@ def tile_share_lstm_cell_t_kernel(
         nc.scalar.dma_start(out=braw[1:2, 0:512], in_=bias_hh.unsqueeze(0))
         nc.scalar.dma_start(out=braw[1:2, 512:768], in_=bias_sh.unsqueeze(0))
         nc.scalar.dma_start(out=m_bf[:], in_=mask.rearrange("(p t) -> p t", t=NT))
-        load_w(0)
+        load_w(0, 0)
+        load_w(0, 1)
         nc.sync.dma_start(out=whh_raw[:, 0:4, :], in_=weight_hh.rearrange("(j p) k -> p j k", p=P))
         nc.sync.dma_start(out=whh_raw[:, 4:6, :], in_=weight_sh.rearrange("(j p) k -> p j k", p=P))
+        load_w(1, 0)
+        load_w(1, 1)
         load_hs(0, 4)
-        load_w(1)
-        load_w(2)
+        load_w(2, 0)
+        load_w(2, 1)
         load_x(0)
         load_x(1)
         load_hs(4, 12)
@@ -323,60 +334,74 @@ def tile_share_lstm_cell_t_kernel(
         for j in range(6):
             nc.tensor.transpose(wt_ps[:, j, :], whh_raw[:, j, :], ident_b[:])
         nc.scalar.copy(out=wT[:], in_=wt_ps[:].rearrange("p j k -> p (j k)"))
-        hs_pe(0, "X1")
-        hs_ev(0, "S")
-        b_ps0 = psum.tile([P, 512], F32, tag="A1", name="b_ps0")
+        w_pe(2, "A1")
+        w_ev(2, "V")
+        b_ps0 = psum.tile([P, 512], F32, tag="P0", name="b_ps0")
         nc.tensor.matmul(out=b_ps0[:], lhsT=ones[:], rhs=braw[:, 0:512], start=True, stop=True)
         nc.scalar.copy(out=bias_bc[:, 0:512], in_=b_ps0[:])
-        b_ps1 = psum.tile([P, 512], F32, tag="X0", name="b_ps1")
+        b_ps1 = psum.tile([P, 512], F32, tag="P1", name="b_ps1")
         nc.tensor.matmul(out=b_ps1[:, 0:256], lhsT=ones[:], rhs=braw[:, 512:768], start=True, stop=True)
         nc.scalar.copy(out=bias_bc[:, 512:768], in_=b_ps1[:, 0:256])
+        w_pe(3, "X1")
+        w_ev(3, "V")
+        w_quant(1)
+        hs_pe(0, "X0")
+        hs_ev(0, "S")
         plain_main(0, 0)
         plain_main(0, 1)
         plain_share(0)
-        hs_pe(1, "X1")
-        hs_ev(1, "S")
-        w_pe(2, "AC")
-        w_ev(2, "V")
-        w_pe(3, "A0")
-        w_ev(3, "V")
-        w_quant(1)
         add_bias(0)
-        w_pe(4, "A1")
+        w_pe(4, "A0")
         w_ev(4, "S")
-        w_pe(5, "X0")
+        w_pe(5, "AC")
         w_ev(5, "S")
         w_quant(2)
-        x_pe(0, "X1")
+        x_pe(0, "A1")
         x_ev(0, "S")
-        x_pe(1, "AC")
+        x_pe(1, "X1")
         x_ev(1, "S")
         quantise(0)
+        hs_pe(1, "AC")
+        hs_ev(1, "S")
+        x_pe(2, "X0")
+        x_ev(2, "S")
+        hs_pe(2, "A1")
+        hs_ev(2, "S")
+        x_pe(3, "X1")
+        x_ev(3, "S")
         plain_main(1, 0)
         plain_main(1, 1)
         plain_share(1)
-        hs_pe(2, "A1")
-        hs_ev(2, "S")
-        x_pe(2, "X0")
-        x_ev(2, "S")
-        x_pe(3, "X1")
-        x_ev(3, "S")
         mx(0)
         nc.gpsimd.tensor_copy(out=m32[:], in_=m_bf[:])
 
-        def group_at(j, off, limit):
-            if (j - off) % 2 == 0 and 0 <= (j - off) // 2 < limit:
-                return (j - off) // 2
-            return -1
+        units = ([(t, 2, t // 2 + 1) for t in range(0, G_FIRST, 2)] + [(t, 4, t // 2 + 2) for t in range(G_FIRST, G_PAIRED, 4)]
+                 + [(t, 2, t // 2 + 1) for t in range(G_PAIRED, G_TILES, 2)])
+
+        def cell_steps(j):
+            for t, n, ready in units:
+                gi = t // 4
+                if j == ready:
+                    if t % 4 == 0:
+                        out_tiles(gi)
+                    cell_sum_gpsimd(gi, t % 4, n)
+                for h in range(n // 2):
+                    if j == ready + 1 + h and t + n < G_TILES:
+                        cell_scalar(t + 2 * h)
+                        cell_scalar(t + 2 * h + 1)
+                        if 2 * h + 2 == n:
+                            store(t, n, 1, nc.sync)
+                if j == ready + 1 + n // 2 and t != V_OUT and t + n < G_TILES:
+                    outputs_gpsimd(gi, t % 4, n)
+                    for which in (0, 2, 3):
+                        store(t, n, which, nc.sync)
 
         bank = 0
         for j in range(NPAIR):
-            if j + 1 < NPAIR:
-                if j > 0:
-                    quantise(j + 1)
+            if j + 2 < NPAIR:
                 add_bias(j + 1)
-                if j == 0:
-                    quantise(j + 1)
+            if j + 1 < NPAIR:
+                quantise(j + 1)
             if 0 <= j - 1:
                 gate_functions(2 * (j - 1), 2)
             if j + 2 < NPAIR:
@@ -393,60 +418,39 @@ def tile_share_lstm_cell_t_kernel(
                 hs_pe(j + 3, "X%d" % (bank % 2))
                 bank = bank + 1
                 hs_ev(j + 3, "S")
-            if j == NPAIR - 1:
-                outputs_vector(2 * j - 6)
-                outputs_vector(2 * j - 5)
             add_mx(j)
             if j + 1 < NPAIR:
                 mx(j + 1)
-            g = group_at(j, 2, NG_OUT)
-            if g >= 0:
-                out_tiles(g)
-                cell_sum_gpsimd(g, 0, 4)
-            g = group_at(j, 3, NG_OUT)
-            if g >= 0:
-                cell_scalar(4 * g)
-                cell_scalar(4 * g + 1)
-            g = group_at(j, 4, NG_OUT)
-            if g >= 0:
-                cell_scalar(4 * g + 2)
-                cell_scalar(4 * g + 3)
-                store(g, 1, 0, 4)
-            g = group_at(j, 5, NG_OUT)
-            if g >= 0:
-                outputs_gpsimd(g)
-                store(g, 0, 0, 4)
-                store(g, 2, 0, 4)
-                store(g, 3, 0, 4)
-            if NG_OUT <= (j - 1) // 2 < NG_SUM:
-                if j % 2 == 1:
-                    out_tiles((j - 1) // 2)
-                cell_sum_gpsimd((j - 1) // 2, 2 * ((j - 1) % 2), 2)
-            if NG_OUT <= (j - 2) // 2 < NG_SUM:
-                cell_scalar(2 * (j - 2))
-                cell_scalar(2 * (j - 2) + 1)
-        g = NG_SUM
-        store(g - 1, 1, 0, 4)
-        out_tiles(g)
-        cell_vector(4 * g)
-        cell_vector(4 * g + 1)
-        gate_functions(4 * g + 2, 1)
-        cell_tanh(4 * g)
-        cell_tanh(4 * g + 1)
-        gate_functions(4 * g + 3, 1)
-        cell_vector(4 * g + 2)
-        cell_tanh(4 * g + 2)
-        outputs_vector(4 * g - 2)
-        outputs_vector(4 * g - 1)
+            if j + 2 == NPAIR:
+                add_bias(j + 1)
+            cell_steps(j)
+        t = G_TILES
+        out_tiles(t // 4)
+        cell_vector(t)
+        cell_vector(t + 1)
+        gate_functions(t + 2, 1)
+        cell_tanh(t)
+        cell_tanh(t + 1)
+        gate_functions(t + 3, 1)
+        cell_scalar(t - 2)
+        cell_scalar(t - 1)
+        outputs_vector(V_OUT)
+        outputs_vector(V_OUT + 1)
         for which in (0, 2, 3):
-            store(g - 1, which, 0, 4)
-        outputs_vector(4 * g)
-        outputs_vector(4 * g + 1)
+            store(V_OUT, 2, which, nc.sync)
+        store(t - 2, 2, 1, nc.sync)
+        outputs_gpsimd(t // 4 - 1, 2, 2)
+        for which in (0, 2, 3):
+            store(t - 2, 2, which, nc.sync)
+        cell_vector(t + 2)
+        cell_tanh(t + 2)
+        outputs_vector(t)
+        outputs_vector(t + 1)
         for which in (1, 0, 2, 3):
-            store(g, which, 0, 2)
-        cell_vector(4 * g + 3)
-        cell_tanh(4 * g + 3)
-        outputs_vector(4 * g + 2)
-        outputs_vector(4 * g + 3)
+            store(t, 2, which, nc.scalar)
+        cell_vector(t + 3)
+        cell_tanh(t + 3)
+        outputs_vector(t + 2)
+        outputs_vector(t + 3)
         for which in (1, 0, 2, 3):
-            store(g, which, 2, 2)
+            store(t + 2, 2, which, nc.scalar)

@@ -18,10 +18,9 @@ H = 128
 NG = 768
 NT = B // P
 NPAIR = NT // 2
-G_TILES = 28
+G_TILES = 24
 G_FIRST = 8
 G_PAIRED = 20
-V_OUT = 24
 
 FLOPS = 2 * B * (D_IN * NG + H * 512 + H * 256)
 BYTES = 2 * (B * D_IN + 3 * B * H + B + NG * D_IN + 768 * H + 2 * NG) + 4 * 4 * B * H
@@ -34,7 +33,7 @@ def tile_share_lstm_cell_t_kernel(
     nc = tc.nc
     with ExitStack() as ctx:
         const = ctx.enter_context(tc.tile_pool(name="const", bufs=1))
-        xpool = ctx.enter_context(tc.tile_pool(name="xpool", bufs=14))
+        xpool = ctx.enter_context(tc.tile_pool(name="xpool", bufs=11))
         gxpool = ctx.enter_context(tc.tile_pool(name="gxpool", bufs=4))
         qpool = ctx.enter_context(tc.tile_pool(name="qpool", bufs=4))
         hspool = ctx.enter_context(tc.tile_pool(name="hspool", bufs=4))
@@ -55,6 +54,7 @@ def tile_share_lstm_cell_t_kernel(
         braw = const.tile([P, NG], BF16)
         m_bf = const.tile([P, NT], BF16)
         m32 = const.tile([P, NT], F32)
+        w_raw = const.tile([P, 6, D_IN], BF16)
         h_sb = const.tile([P, NT, H], BF16)
         s_sb = const.tile([P, NT, H], BF16)
         c_sb = const.tile([P, NT, H], BF16)
@@ -67,7 +67,6 @@ def tile_share_lstm_cell_t_kernel(
         w_codes = const.tile([P, 2 * NG], U32, align_bytes=64)
         w_scales = const.tile([P, 2 * NG], U8, align_bytes=64)
 
-        w_raw_t = {}
         w_grp_t = {}
         xp_t = {}
         ps_t = {}
@@ -83,11 +82,8 @@ def tile_share_lstm_cell_t_kernel(
             nc.sync.dma_start(out=x_sb[:], in_=xv[:, 2 * k:2 * k + 2, :])
             xp_t[k] = x_sb
 
-        def load_w(a, j):
-            if j == 0:
-                w_sb = xpool.tile([P, 2, D_IN], BF16, name="x_sb")
-                w_raw_t[a] = w_sb
-            nc.sync.dma_start(out=w_raw_t[a][:, j, :], in_=wv[:, 2 * a + j, :])
+        def load_w(lo, n):
+            nc.sync.dma_start(out=w_raw[:, lo:lo + n, :], in_=wv[:, lo:lo + n, :])
 
         def load_hs(lo, n):
             nc.sync.dma_start(out=h_sb[:, lo:lo + n, :], in_=hv[:, lo:lo + n, :])
@@ -115,7 +111,7 @@ def tile_share_lstm_cell_t_kernel(
         def w_pe(j, tag):
             w_ps = psum.tile([P, 4, P], F32, tag=tag, name="w_ps")
             ps_t["w", j] = w_ps
-            ww = w_raw_t[j // 2][:, j % 2, :].bitcast(F32)
+            ww = w_raw[:, j, :].bitcast(F32)
             for q in range(4):
                 nc.tensor.transpose(w_ps[:, q, :], ww[:, 256 * (q // 2) + q % 2:256 * (q // 2) + 256:2], ident_f[:])
 
@@ -248,8 +244,7 @@ def tile_share_lstm_cell_t_kernel(
             m = m32[:, t:t + 1]
             nc.scalar.activation(out=g4[:, tt, 128:256], in_=g4[:, tt, 0:128], func=ACT.Tanh, scale=m)
             nc.scalar.activation(out=oc[:, tt, :], in_=g4[:, tt, 0:128], func=ACT.Copy, scale=m)
-            if t < V_OUT or t >= V_OUT + 2:
-                nc.scalar.activation(out=g4[:, tt, 384:512], in_=g4[:, tt, 128:256], func=ACT.Copy, scale=m)
+            nc.scalar.activation(out=g4[:, tt, 384:512], in_=g4[:, tt, 128:256], func=ACT.Copy, scale=m)
 
         def outputs_gpsimd(gi, lo, n):
             g4 = g4_t[gi]
@@ -261,15 +256,16 @@ def tile_share_lstm_cell_t_kernel(
                 in1=g4[:, lo:lo + n, 384:512].unsqueeze(2).to_broadcast([P, n, 2, H]), op=ALU.mult,
             )
 
-        def cell_vector(t):
+        def cell_vector(t, n):
             gi = t // 4
-            tt = t % 4
             g4 = g4_t[gi]
-            oc = out_t[gi][1]
-            m = m32[:, t:t + 1]
-            nc.vector.scalar_tensor_tensor(out=g4[:, tt, 128:256], in0=c_sb[:, t, :], scalar=m, in1=g4[:, tt, 128:256], op0=ALU.mult, op1=ALU.mult)
-            nc.vector.scalar_tensor_tensor(out=g4[:, tt, 384:512], in0=g4[:, tt, 384:512], scalar=m, in1=g4[:, tt, 0:128], op0=ALU.mult, op1=ALU.mult)
-            nc.vector.tensor_tensor(out=oc[:, tt, :], in0=g4[:, tt, 128:256], in1=g4[:, tt, 384:512], op=ALU.add)
+            tiles = [(t + i, t % 4 + i) for i in range(n)]
+            for ti, tt in tiles:
+                nc.vector.scalar_tensor_tensor(out=g4[:, tt, 128:256], in0=c_sb[:, ti, :], scalar=m32[:, ti:ti + 1], in1=g4[:, tt, 128:256], op0=ALU.mult, op1=ALU.mult)
+            for ti, tt in tiles:
+                nc.vector.scalar_tensor_tensor(out=g4[:, tt, 384:512], in0=g4[:, tt, 384:512], scalar=m32[:, ti:ti + 1], in1=g4[:, tt, 0:128], op0=ALU.mult, op1=ALU.mult)
+            for ti, tt in tiles:
+                nc.vector.tensor_tensor(out=out_t[gi][1][:, tt, :], in0=g4[:, tt, 128:256], in1=g4[:, tt, 384:512], op=ALU.add)
 
         def cell_tanh(t):
             gi = t // 4
@@ -296,34 +292,41 @@ def tile_share_lstm_cell_t_kernel(
             eng.dma_start(out=outs[which][:, t:t + n, :], in_=src[:, lo:lo + n, :])
 
 
-        nc.vector.memset(ones[:], 1.0)
         nc.vector.memset(braw[:], 0.0)
+        nc.vector.memset(ones[:], 1.0)
         nc.scalar.activation(out=warm[:], in_=ones[:, 0:8], func=ACT.Sigmoid)
         make_identity(nc, ident_f[:])
         make_identity(nc, ident_b[:])
-        nc.scalar.dma_start(out=braw[0:1, :], in_=bias_ih.unsqueeze(0))
-        nc.scalar.dma_start(out=braw[1:2, 0:512], in_=bias_hh.unsqueeze(0))
-        nc.scalar.dma_start(out=braw[1:2, 512:768], in_=bias_sh.unsqueeze(0))
-        nc.scalar.dma_start(out=m_bf[:], in_=mask.rearrange("(p t) -> p t", t=NT))
-        load_w(0, 0)
         load_w(0, 1)
+        load_w(1, 1)
         nc.sync.dma_start(out=whh_raw[:, 0:4, :], in_=weight_hh.rearrange("(j p) k -> p j k", p=P))
         nc.sync.dma_start(out=whh_raw[:, 4:6, :], in_=weight_sh.rearrange("(j p) k -> p j k", p=P))
-        load_w(1, 0)
-        load_w(1, 1)
+        load_w(2, 2)
+        nc.sync.dma_start(out=braw[0:1, :], in_=bias_ih.unsqueeze(0))
+        nc.sync.dma_start(out=braw[1:2, 0:512], in_=bias_hh.unsqueeze(0))
+        nc.sync.dma_start(out=braw[1:2, 512:768], in_=bias_sh.unsqueeze(0))
         load_hs(0, 4)
-        load_w(2, 0)
-        load_w(2, 1)
+        load_w(4, 2)
         load_x(0)
         load_x(1)
         load_hs(4, 12)
         load_x(2)
         load_x(3)
         nc.sync.dma_start(out=c_sb[:], in_=cv)
+        nc.sync.dma_start(out=m_bf[:], in_=mask.rearrange("(p t) -> p t", t=NT))
         load_x(4)
         load_hs(16, 16)
-        for k in range(5, NPAIR):
-            load_x(k)
+        load_x(5)
+        load_x(6)
+        load_x(7)
+        load_x(8)
+        load_x(9)
+        load_x(10)
+        load_x(11)
+        load_x(12)
+        load_x(13)
+        load_x(14)
+        load_x(15)
 
         w_pe(0, "AC")
         w_ev(0, "V")
@@ -378,23 +381,32 @@ def tile_share_lstm_cell_t_kernel(
         units = ([(t, 2, t // 2 + 1) for t in range(0, G_FIRST, 2)] + [(t, 4, t // 2 + 2) for t in range(G_FIRST, G_PAIRED, 4)]
                  + [(t, 2, t // 2 + 1) for t in range(G_PAIRED, G_TILES, 2)])
 
-        def cell_steps(j):
+        def cell_scalars(j):
+            for t, n, ready in units:
+                for h in range(n // 2):
+                    if j == ready + 1 + h:
+                        cell_scalar(t + 2 * h)
+                        cell_scalar(t + 2 * h + 1)
+                        if 2 * h + 2 == n:
+                            store(t, n, 1, nc.sync)
+
+        def cell_gpsimd(j):
             for t, n, ready in units:
                 gi = t // 4
                 if j == ready:
                     if t % 4 == 0:
                         out_tiles(gi)
                     cell_sum_gpsimd(gi, t % 4, n)
-                for h in range(n // 2):
-                    if j == ready + 1 + h and t + n < G_TILES:
-                        cell_scalar(t + 2 * h)
-                        cell_scalar(t + 2 * h + 1)
-                        if 2 * h + 2 == n:
-                            store(t, n, 1, nc.sync)
-                if j == ready + 1 + n // 2 and t != V_OUT and t + n < G_TILES:
+                if j == ready + 1 + 0 + n // 2:
                     outputs_gpsimd(gi, t % 4, n)
                     for which in (0, 2, 3):
                         store(t, n, which, nc.sync)
+
+        def outputs_v(k, eng):
+            outputs_vector(2 * k)
+            outputs_vector(2 * k + 1)
+            for which in (0, 2, 3):
+                store(2 * k, 2, which, eng)
 
         bank = 0
         for j in range(NPAIR):
@@ -423,34 +435,24 @@ def tile_share_lstm_cell_t_kernel(
                 mx(j + 1)
             if j + 2 == NPAIR:
                 add_bias(j + 1)
-            cell_steps(j)
-        t = G_TILES
-        out_tiles(t // 4)
-        cell_vector(t)
-        cell_vector(t + 1)
-        gate_functions(t + 2, 1)
-        cell_tanh(t)
-        cell_tanh(t + 1)
-        gate_functions(t + 3, 1)
-        cell_scalar(t - 2)
-        cell_scalar(t - 1)
-        outputs_vector(V_OUT)
-        outputs_vector(V_OUT + 1)
-        for which in (0, 2, 3):
-            store(V_OUT, 2, which, nc.sync)
-        store(t - 2, 2, 1, nc.sync)
-        outputs_gpsimd(t // 4 - 1, 2, 2)
-        for which in (0, 2, 3):
-            store(t - 2, 2, which, nc.sync)
-        cell_vector(t + 2)
-        cell_tanh(t + 2)
-        outputs_vector(t)
-        outputs_vector(t + 1)
-        for which in (1, 0, 2, 3):
-            store(t, 2, which, nc.scalar)
-        cell_vector(t + 3)
-        cell_tanh(t + 3)
-        outputs_vector(t + 2)
-        outputs_vector(t + 3)
-        for which in (1, 0, 2, 3):
-            store(t + 2, 2, which, nc.scalar)
+            cell_gpsimd(j)
+            if j + 1 < NPAIR:
+                cell_scalars(j)
+        last = NPAIR - 1
+        first = G_TILES // 2
+        gate_functions(2 * last, 2)
+        for k in range(first, last + 1):
+            if k % 2 == 0:
+                out_tiles(k // 2)
+            cell_vector(2 * k, 2)
+            cell_tanh(2 * k)
+            cell_tanh(2 * k + 1)
+            store(2 * k, 2, 1, nc.sync)
+            if k == first:
+                for j in range(last, last + 4):
+                    cell_scalars(j)
+                    cell_gpsimd(j + 1)
+            if k - 1 >= first:
+                outputs_v(k - 1, nc.sync)
+        for k in range(last + 1 - 1, last + 1):
+            outputs_v(k, nc.scalar)

@@ -19,8 +19,8 @@ NG = 768
 NT = B // P
 NPAIR = NT // 2
 G_TILES = 24
-G_FIRST = 8
-G_PAIRED = 20
+G_FIRST = 0
+G_PAIRED = 24
 
 FLOPS = 2 * B * (D_IN * NG + H * 512 + H * 256)
 BYTES = 2 * (B * D_IN + 3 * B * H + B + NG * D_IN + 768 * H + 2 * NG) + 4 * 4 * B * H
@@ -60,7 +60,7 @@ def tile_share_lstm_cell_t_kernel(
         c_sb = const.tile([P, NT, H], BF16)
         ident_f = const.tile([P, P], F32)
         ident_b = const.tile([P, P], BF16)
-        ones = const.tile([P, P], BF16)
+        ones = const.tile([P, 512], BF16)
         warm = const.tile([P, 8], F32)
         wT = const.tile([P, NG], BF16)
         bias_bc = const.tile([P, NG], F32)
@@ -94,6 +94,11 @@ def tile_share_lstm_cell_t_kernel(
                 nc.vector.tensor_copy(out=out, in_=in_)
             else:
                 nc.scalar.copy(out=out, in_=in_)
+
+        def keep_warm(n, tag):
+            for i in range(n):
+                idle_ps = psum.tile([P, 512], F32, tag=tag, name="idle_ps")
+                nc.tensor.matmul(out=idle_ps[:], lhsT=ones[:, 0:P], rhs=ones[:], start=True, stop=True)
 
         def hs_pe(k, tag):
             hs_ps = psum.tile([P, 2, 2, H], BF16, tag=tag, name="hs_ps")
@@ -292,8 +297,8 @@ def tile_share_lstm_cell_t_kernel(
             eng.dma_start(out=outs[which][:, t:t + n, :], in_=src[:, lo:lo + n, :])
 
 
+        nc.gpsimd.memset(ones[:], 1.0)
         nc.vector.memset(braw[:], 0.0)
-        nc.vector.memset(ones[:], 1.0)
         nc.scalar.activation(out=warm[:], in_=ones[:, 0:8], func=ACT.Sigmoid)
         make_identity(nc, ident_f[:])
         make_identity(nc, ident_b[:])
@@ -328,11 +333,13 @@ def tile_share_lstm_cell_t_kernel(
         load_x(14)
         load_x(15)
 
+        keep_warm(3, "P0")
         w_pe(0, "AC")
         w_ev(0, "V")
         w_pe(1, "A0")
         w_ev(1, "V")
         w_quant(0)
+        keep_warm(1, "P0")
         wt_ps = psum.tile([P, 6, H], BF16, tag="X0", name="wt_ps")
         for j in range(6):
             nc.tensor.transpose(wt_ps[:, j, :], whh_raw[:, j, :], ident_b[:])
@@ -340,23 +347,25 @@ def tile_share_lstm_cell_t_kernel(
         w_pe(2, "A1")
         w_ev(2, "V")
         b_ps0 = psum.tile([P, 512], F32, tag="P0", name="b_ps0")
-        nc.tensor.matmul(out=b_ps0[:], lhsT=ones[:], rhs=braw[:, 0:512], start=True, stop=True)
+        nc.tensor.matmul(out=b_ps0[:], lhsT=ones[:, 0:P], rhs=braw[:, 0:512], start=True, stop=True)
         nc.scalar.copy(out=bias_bc[:, 0:512], in_=b_ps0[:])
         b_ps1 = psum.tile([P, 512], F32, tag="P1", name="b_ps1")
-        nc.tensor.matmul(out=b_ps1[:, 0:256], lhsT=ones[:], rhs=braw[:, 512:768], start=True, stop=True)
+        nc.tensor.matmul(out=b_ps1[:, 0:256], lhsT=ones[:, 0:P], rhs=braw[:, 512:768], start=True, stop=True)
         nc.scalar.copy(out=bias_bc[:, 512:768], in_=b_ps1[:, 0:256])
         w_pe(3, "X1")
         w_ev(3, "V")
         w_quant(1)
         hs_pe(0, "X0")
         hs_ev(0, "S")
+        hs_pe(1, "AC")
+        hs_ev(1, "S")
         plain_main(0, 0)
         plain_main(0, 1)
         plain_share(0)
         add_bias(0)
         w_pe(4, "A0")
         w_ev(4, "S")
-        w_pe(5, "AC")
+        w_pe(5, "X0")
         w_ev(5, "S")
         w_quant(2)
         x_pe(0, "A1")
@@ -364,17 +373,16 @@ def tile_share_lstm_cell_t_kernel(
         x_pe(1, "X1")
         x_ev(1, "S")
         quantise(0)
-        hs_pe(1, "AC")
-        hs_ev(1, "S")
+        plain_main(1, 0)
+        plain_main(1, 1)
+        plain_share(1)
+        add_bias(1)
         x_pe(2, "X0")
         x_ev(2, "S")
         hs_pe(2, "A1")
         hs_ev(2, "S")
         x_pe(3, "X1")
         x_ev(3, "S")
-        plain_main(1, 0)
-        plain_main(1, 1)
-        plain_share(1)
         mx(0)
         nc.gpsimd.tensor_copy(out=m32[:], in_=m_bf[:])
 
@@ -408,37 +416,35 @@ def tile_share_lstm_cell_t_kernel(
             for which in (0, 2, 3):
                 store(2 * k, 2, which, eng)
 
-        bank = 0
+        last = NPAIR - 1
         for j in range(NPAIR):
-            if j + 2 < NPAIR:
+            k = j + 2
+            if 0 < j < last - 1:
                 add_bias(j + 1)
-            if j + 1 < NPAIR:
+            if j < last:
                 quantise(j + 1)
-            if 0 <= j - 1:
+            if j > 0:
                 gate_functions(2 * (j - 1), 2)
-            if j + 2 < NPAIR:
-                k = j + 2
+            if k < NPAIR:
                 plain_main(k, 0)
-                x_pe(2 * k, "X%d" % (bank % 2))
+                x_pe(2 * k, "X%d" % (3 * j % 2))
                 plain_main(k, 1)
-                x_pe(2 * k + 1, "X%d" % ((bank + 1) % 2))
+                x_pe(2 * k + 1, "X%d" % ((3 * j + 1) % 2))
                 plain_share(k)
-                bank = bank + 2
+            if k < NPAIR:
                 x_ev(2 * k, "S")
                 x_ev(2 * k + 1, "S")
             if j + 3 < NPAIR:
-                hs_pe(j + 3, "X%d" % (bank % 2))
-                bank = bank + 1
+                hs_pe(j + 3, "X%d" % (3 * j % 2))
+            cell_scalars(j)
+            if j + 3 < NPAIR:
                 hs_ev(j + 3, "S")
             add_mx(j)
-            if j + 1 < NPAIR:
+            if j < last:
                 mx(j + 1)
-            if j + 2 == NPAIR:
+            if j == last - 1:
                 add_bias(j + 1)
             cell_gpsimd(j)
-            if j + 1 < NPAIR:
-                cell_scalars(j)
-        last = NPAIR - 1
         first = G_TILES // 2
         gate_functions(2 * last, 2)
         for k in range(first, last + 1):

@@ -60,7 +60,7 @@ def tile_share_lstm_cell_t_kernel(
         c_sb = const.tile([P, NT, H], BF16)
         ident_f = const.tile([P, P], F32)
         ident_b = const.tile([P, P], BF16)
-        ones = const.tile([P, 512], BF16)
+        ones = const.tile([P, P], BF16)
         warm = const.tile([P, 8], F32)
         wT = const.tile([P, NG], BF16)
         bias_bc = const.tile([P, NG], F32)
@@ -96,9 +96,9 @@ def tile_share_lstm_cell_t_kernel(
                 nc.scalar.copy(out=out, in_=in_)
 
         def keep_warm(n, tag):
+            idle_ps = psum.tile([P, 4, P], F32, tag=tag, name="idle_ps")
             for i in range(n):
-                idle_ps = psum.tile([P, 512], F32, tag=tag, name="idle_ps")
-                nc.tensor.matmul(out=idle_ps[:], lhsT=ones[:, 0:P], rhs=ones[:], start=True, stop=True)
+                nc.tensor.matmul(out=idle_ps[:, i % 4, :], lhsT=ones[:], rhs=ones[:], start=True, stop=True)
 
         def hs_pe(k, tag):
             hs_ps = psum.tile([P, 2, 2, H], BF16, tag=tag, name="hs_ps")
@@ -255,11 +255,10 @@ def tile_share_lstm_cell_t_kernel(
             g4 = g4_t[gi]
             oh, oc, os_ = out_t[gi]
             nc.gpsimd.tensor_tensor(out=oh[:, lo:lo + n, :], in0=g4[:, lo:lo + n, 256:384], in1=g4[:, lo:lo + n, 384:512], op=ALU.mult)
-            nc.gpsimd.tensor_tensor(
-                out=os_[:, :, lo:lo + n, :].rearrange("p k t c -> p t k c"),
-                in0=g4[:, lo:lo + n, 512:768].rearrange("p t (k c) -> p t k c", k=2),
-                in1=g4[:, lo:lo + n, 384:512].unsqueeze(2).to_broadcast([P, n, 2, H]), op=ALU.mult,
-            )
+            for s in range(2):
+                nc.gpsimd.tensor_tensor(
+                    out=os_[:, s, lo:lo + n, :], in0=g4[:, lo:lo + n, 512 + H * s:512 + H * s + H], in1=g4[:, lo:lo + n, 384:512], op=ALU.mult,
+                )
 
         def cell_vector(t, n):
             gi = t // 4
@@ -297,7 +296,7 @@ def tile_share_lstm_cell_t_kernel(
             eng.dma_start(out=outs[which][:, t:t + n, :], in_=src[:, lo:lo + n, :])
 
 
-        nc.gpsimd.memset(ones[:], 1.0)
+        nc.vector.memset(ones[:], 1.0)
         nc.vector.memset(braw[:], 0.0)
         nc.scalar.activation(out=warm[:], in_=ones[:, 0:8], func=ACT.Sigmoid)
         make_identity(nc, ident_f[:])
@@ -333,13 +332,14 @@ def tile_share_lstm_cell_t_kernel(
         load_x(14)
         load_x(15)
 
-        keep_warm(3, "P0")
+        keep_warm(15, "P0")
         w_pe(0, "AC")
         w_ev(0, "V")
+        keep_warm(4, "P0")
         w_pe(1, "A0")
         w_ev(1, "V")
         w_quant(0)
-        keep_warm(1, "P0")
+        keep_warm(4, "P0")
         wt_ps = psum.tile([P, 6, H], BF16, tag="X0", name="wt_ps")
         for j in range(6):
             nc.tensor.transpose(wt_ps[:, j, :], whh_raw[:, j, :], ident_b[:])
@@ -347,14 +347,15 @@ def tile_share_lstm_cell_t_kernel(
         w_pe(2, "A1")
         w_ev(2, "V")
         b_ps0 = psum.tile([P, 512], F32, tag="P0", name="b_ps0")
-        nc.tensor.matmul(out=b_ps0[:], lhsT=ones[:, 0:P], rhs=braw[:, 0:512], start=True, stop=True)
+        nc.tensor.matmul(out=b_ps0[:], lhsT=ones[:], rhs=braw[:, 0:512], start=True, stop=True)
         nc.scalar.copy(out=bias_bc[:, 0:512], in_=b_ps0[:])
         b_ps1 = psum.tile([P, 512], F32, tag="P1", name="b_ps1")
-        nc.tensor.matmul(out=b_ps1[:, 0:256], lhsT=ones[:, 0:P], rhs=braw[:, 512:768], start=True, stop=True)
+        nc.tensor.matmul(out=b_ps1[:, 0:256], lhsT=ones[:], rhs=braw[:, 512:768], start=True, stop=True)
         nc.scalar.copy(out=bias_bc[:, 512:768], in_=b_ps1[:, 0:256])
         w_pe(3, "X1")
         w_ev(3, "V")
         w_quant(1)
+        keep_warm(4, "PC")
         hs_pe(0, "X0")
         hs_ev(0, "S")
         hs_pe(1, "AC")

from contextlib import ExitStack

import concourse.mybir as mybir
from concourse.masks import make_identity

F32 = mybir.dt.float32
BF16 = mybir.dt.bfloat16
U32 = mybir.dt.uint32
U8 = mybir.dt.uint8
FP8X4 = mybir.dt.float8_e4m3fn_x4
ACT = mybir.ActivationFunctionType
ALU = mybir.AluOpType

P = 128
B = 4096
D_IN = 1024
H = 128
NG = 768
NT = B // P
NPAIR = NT // 2
G_TILES = 24
G_FIRST = 0
G_PAIRED = 24

FLOPS = 2 * B * (D_IN * NG + H * 512 + H * 256)
BYTES = 2 * (B * D_IN + 3 * B * H + B + NG * D_IN + 768 * H + 2 * NG) + 4 * 4 * B * H


def tile_share_lstm_cell_t_kernel(
    tc, x_in, h_minors, c_minors, s_minors, mask, weight_ih, weight_hh, weight_sh,
    bias_ih, bias_hh, bias_sh, idx, out_0, out_1, out_2, out_3,
):
    nc = tc.nc
    with ExitStack() as ctx:
        const = ctx.enter_context(tc.tile_pool(name="const", bufs=1))
        xpool = ctx.enter_context(tc.tile_pool(name="xpool", bufs=11))
        gxpool = ctx.enter_context(tc.tile_pool(name="gxpool", bufs=4))
        qpool = ctx.enter_context(tc.tile_pool(name="qpool", bufs=4))
        hspool = ctx.enter_context(tc.tile_pool(name="hspool", bufs=4))
        pbpool = ctx.enter_context(tc.tile_pool(name="pbpool", bufs=3))
        gpool = ctx.enter_context(tc.tile_pool(name="gpool", bufs=5))
        opool = ctx.enter_context(tc.tile_pool(name="opool", bufs=3))
        psum = ctx.enter_context(tc.psum_pool(name="psum", bufs=1))
        ctx.enter_context(tc.manual_schedule())

        xv = x_in.rearrange("(p t) k -> p t k", t=NT)
        hv = h_minors.rearrange("(p t) k -> p t k", t=NT)
        cv = c_minors.rearrange("(p t) k -> p t k", t=NT)
        sv = s_minors[idx].rearrange("(p t) k -> p t k", t=NT)
        wv = weight_ih.rearrange("(j p) k -> p j k", p=P)
        outs = [o.rearrange("(p t) k -> p t k", t=NT) for o in (out_0, out_1, out_2, out_3)]

        whh_raw = const.tile([P, 6, H], BF16)
        braw = const.tile([P, NG], BF16)
        m_bf = const.tile([P, NT], BF16)
        m32 = const.tile([P, NT], F32)
        w_raw = const.tile([P, 6, D_IN], BF16)
        h_sb = const.tile([P, NT, H], BF16)
        s_sb = const.tile([P, NT, H], BF16)
        c_sb = const.tile([P, NT, H], BF16)
        ident_f = const.tile([P, P], F32)
        ident_b = const.tile([P, P], BF16)
        ones = const.tile([P, P], BF16)
        warm = const.tile([P, 8], F32)
        wT = const.tile([P, NG], BF16)
        bias_bc = const.tile([P, NG], F32)
        w_codes = const.tile([P, 2 * NG], U32, align_bytes=64)
        w_scales = const.tile([P, 2 * NG], U8, align_bytes=64)

        w_grp_t = {}
        xp_t = {}
        ps_t = {}
        xg_t = {}
        xq_t = {}
        hsT_t = {}
        pb_t = {}
        g4_t = {}
        out_t = {}

        def load_x(k):
            x_sb = xpool.tile([P, 2, D_IN], BF16, name="x_sb")
            nc.sync.dma_start(out=x_sb[:], in_=xv[:, 2 * k:2 * k + 2, :])
            xp_t[k] = x_sb

        def load_w(lo, n):
            nc.sync.dma_start(out=w_raw[:, lo:lo + n, :], in_=wv[:, lo:lo + n, :])

        def load_hs(lo, n):
            nc.sync.dma_start(out=h_sb[:, lo:lo + n, :], in_=hv[:, lo:lo + n, :])
            nc.sync.dma_start(out=s_sb[:, lo:lo + n, :], in_=sv[:, lo:lo + n, :])

        def copy_out(eng, out, in_):
            if eng == "V":
                nc.vector.tensor_copy(out=out, in_=in_)
            else:
                nc.scalar.copy(out=out, in_=in_)

        def keep_warm(n, tag):
            idle_ps = psum.tile([P, 4, P], F32, tag=tag, name="idle_ps")
            for i in range(n):
                nc.tensor.matmul(out=idle_ps[:, i % 4, :], lhsT=ones[:], rhs=ones[:], start=True, stop=True)

        def hs_pe(k, tag):
            hs_ps = psum.tile([P, 2, 2, H], BF16, tag=tag, name="hs_ps")
            ps_t["hs", k] = hs_ps
            for tt in range(2):
                nc.tensor.transpose(hs_ps[:, 0, tt, :], h_sb[:, 2 * k + tt, :], ident_b[:])
            for tt in range(2):
                nc.tensor.transpose(hs_ps[:, 1, tt, :], s_sb[:, 2 * k + tt, :], ident_b[:])

        def hs_ev(k, eng):
            hsT = hspool.tile([P, 2, 2, H], BF16, name="hsT")
            hsT_t[k] = hsT
            copy_out(eng, hsT[:], ps_t["hs", k][:])

        def w_pe(j, tag):
            w_ps = psum.tile([P, 4, P], F32, tag=tag, name="w_ps")
            ps_t["w", j] = w_ps
            ww = w_raw[:, j, :].bitcast(F32)
            for q in range(4):
                nc.tensor.transpose(w_ps[:, q, :], ww[:, 256 * (q // 2) + q % 2:256 * (q // 2) + 256:2], ident_f[:])

        def w_ev(j, eng):
            if j % 2 == 0:
                w_grp = gxpool.tile([P, 2, 2 * P, 2], F32, align_bytes=64, name="xg")
                w_grp_t[j // 2] = w_grp
            lo = P * (j % 2)
            copy_out(eng, w_grp_t[j // 2][:, :, lo:lo + P, :], ps_t["w", j][:].rearrange("p (g u) r -> p g r u", g=2))

        def w_quant(a):
            for g in range(2):
                lo = g * NG + 256 * a
                nc.vector.quantize_mx(
                    out=w_codes[:, lo:lo + 256].bitcast(FP8X4), scales=w_scales[:, lo:lo + 256],
                    in_=w_grp_t[a][:, g].rearrange("p n u -> p (n u)").bitcast(BF16),
                )

        def x_pe(t, tag):
            xt = psum.tile([P, 4, P], F32, tag=tag, name="xt")
            ps_t["x", t] = xt
            xw = xp_t[t // 2][:, t % 2, :].bitcast(F32)
            for q in range(4):
                nc.tensor.transpose(xt[:, q, :], xw[:, 256 * (q // 2) + q % 2:256 * (q // 2) + 256:2], ident_f[:])

        def x_ev(t, eng):
            k = t // 2
            if t % 2 == 0:
                xg_new = gxpool.tile([P, 2, 2, P, 2], F32, align_bytes=64, name="xg")
                xg_t[k] = xg_new
            copy_out(eng, xg_t[k][:, t % 2], ps_t["x", t][:].rearrange("p (g u) r -> p g r u", g=2))

        def quantise(k):
            xc = qpool.tile([P, 512], U32, align_bytes=64, name="xc")
            xs = qpool.tile([P, 512], U8, align_bytes=64, name="xs")
            xq_t[k] = (xc, xs)
            nc.vector.quantize_mx(
                out=xc[:].bitcast(FP8X4), scales=xs[:],
                in_=xg_t[k][:].rearrange("p t g r u -> p (t g r u)").bitcast(BF16),
            )

        def plain_main(k, i):
            p_ps = psum.tile([P, 512], F32, tag="P%d" % i, name="p_ps")
            ps_t["p", k, i] = p_ps
            nc.tensor.matmul(out=p_ps[:], lhsT=hsT_t[k][:, 0, i, :], rhs=wT[:, 0:512], start=True, stop=True)

        def plain_share(k):
            pc = psum.tile([P, 512], F32, tag="PC", name="pc")
            ps_t["pc", k] = pc
            for i in range(2):
                nc.tensor.matmul(out=pc[:, 256 * i:256 * i + 256], lhsT=hsT_t[k][:, 1, i, :], rhs=wT[:, 512:768], start=True, stop=True)

        def add_bias(k):
            pb = pbpool.tile([P, 2, NG], F32, name="pb")
            pb_t[k] = pb
            for i in range(2):
                nc.vector.tensor_tensor(out=pb[:, i, 0:512], in0=ps_t["p", k, i][:], in1=bias_bc[:, 0:512], op=ALU.add)
            nc.vector.tensor_tensor(
                out=pb[:, :, 512:768], in0=ps_t["pc", k][:].rearrange("p (t n) -> p t n", t=2),
                in1=bias_bc[:, 512:768].unsqueeze(1).to_broadcast([P, 2, 256]), op=ALU.add,
            )

        def mx(k):
            xc, xs = xq_t[k]
            a0 = psum.tile([P, 512], F32, tag="A0", name="a0")
            a1 = psum.tile([P, 512], F32, tag="A1", name="a1")
            ac = psum.tile([P, 512], F32, tag="AC", name="ac")
            ps_t["mx", k] = (a0, a1, ac)
            mx_main(k, 0, a0)
            for i in range(2):
                for g in range(2):
                    lo = (2 * i + g) * P
                    nc.tensor.matmul_mx(
                        out=ac[:, 256 * i:256 * i + 256], lhsT=xc[:, lo:lo + P].bitcast(FP8X4), lhsT_scale=xs[:, lo:lo + P],
                        rhs=w_codes[:, g * NG + 512:g * NG + 768].bitcast(FP8X4), rhs_scale=w_scales[:, g * NG + 512:g * NG + 768],
                        start=(g == 0), stop=(g == 1),
                    )
            mx_main(k, 1, a1)

        def mx_main(k, i, dst):
            xc, xs = xq_t[k]
            for g in range(2):
                lo = (2 * i + g) * P
                nc.tensor.matmul_mx(
                    out=dst[:], lhsT=xc[:, lo:lo + P].bitcast(FP8X4), lhsT_scale=xs[:, lo:lo + P],
                    rhs=w_codes[:, g * NG:g * NG + 512].bitcast(FP8X4), rhs_scale=w_scales[:, g * NG:g * NG + 512],
                    start=(g == 0), stop=(g == 1),
                )

        def add_mx(k):
            gi = k // 2
            tt = 2 * (k % 2)
            if tt == 0:
                g4_new = gpool.tile([P, 4, NG], F32, name="g4")
                g4_t[gi] = g4_new
            g4 = g4_t[gi]
            a0, a1, ac = ps_t["mx", k]
            pb = pb_t[k]
            nc.vector.tensor_tensor(out=g4[:, tt, 0:512], in0=a0[:], in1=pb[:, 0, 0:512], op=ALU.add)
            nc.vector.tensor_tensor(
                out=g4[:, tt:tt + 2, 512:768], in0=ac[:].rearrange("p (t n) -> p t n", t=2),
                in1=pb[:, :, 512:768], op=ALU.add,
            )
            nc.vector.tensor_tensor(out=g4[:, tt + 1, 0:512], in0=a1[:], in1=pb[:, 1, 0:512], op=ALU.add)

        def gate_functions(t, n):
            g4 = g4_t[t // 4]
            tt = t % 4
            nc.scalar.activation(out=g4[:, tt:tt + n, 0:384], in_=g4[:, tt:tt + n, 0:384], func=ACT.Sigmoid)
            nc.scalar.activation(out=g4[:, tt:tt + n, 384:512], in_=g4[:, tt:tt + n, 384:512], func=ACT.Tanh)
            nc.scalar.activation(out=g4[:, tt:tt + n, 512:768], in_=g4[:, tt:tt + n, 512:768], func=ACT.Sigmoid)

        def out_tiles(gi):
            oh = opool.tile([P, 4, H], F32, name="oh")
            oc = opool.tile([P, 4, H], F32, name="oc")
            os_ = opool.tile([P, 2, 4, H], F32, name="os_")
            out_t[gi] = (oh, oc, os_)

        def cell_sum_gpsimd(gi, lo, n):
            g4 = g4_t[gi]
            nc.gpsimd.tensor_tensor(out=g4[:, lo:lo + n, 128:256], in0=g4[:, lo:lo + n, 128:256], in1=c_sb[:, 4 * gi + lo:4 * gi + lo + n, :], op=ALU.mult)
            nc.gpsimd.tensor_tensor(out=g4[:, lo:lo + n, 384:512], in0=g4[:, lo:lo + n, 0:128], in1=g4[:, lo:lo + n, 384:512], op=ALU.mult)
            nc.gpsimd.tensor_tensor(out=g4[:, lo:lo + n, 0:128], in0=g4[:, lo:lo + n, 128:256], in1=g4[:, lo:lo + n, 384:512], op=ALU.add)

        def cell_scalar(t):
            gi = t // 4
            tt = t % 4
            g4 = g4_t[gi]
            oc = out_t[gi][1]
            m = m32[:, t:t + 1]
            nc.scalar.activation(out=g4[:, tt, 128:256], in_=g4[:, tt, 0:128], func=ACT.Tanh, scale=m)
            nc.scalar.activation(out=oc[:, tt, :], in_=g4[:, tt, 0:128], func=ACT.Copy, scale=m)
            nc.scalar.activation(out=g4[:, tt, 384:512], in_=g4[:, tt, 128:256], func=ACT.Copy, scale=m)

        def outputs_gpsimd(gi, lo, n):
            g4 = g4_t[gi]
            oh, oc, os_ = out_t[gi]
            nc.gpsimd.tensor_tensor(out=oh[:, lo:lo + n, :], in0=g4[:, lo:lo + n, 256:384], in1=g4[:, lo:lo + n, 384:512], op=ALU.mult)
            for s in range(2):
                nc.gpsimd.tensor_tensor(
                    out=os_[:, s, lo:lo + n, :], in0=g4[:, lo:lo + n, 512 + H * s:512 + H * s + H], in1=g4[:, lo:lo + n, 384:512], op=ALU.mult,
                )

        def cell_vector(t, n):
            gi = t // 4
            g4 = g4_t[gi]
            tiles = [(t + i, t % 4 + i) for i in range(n)]
            for ti, tt in tiles:
                nc.vector.scalar_tensor_tensor(out=g4[:, tt, 128:256], in0=c_sb[:, ti, :], scalar=m32[:, ti:ti + 1], in1=g4[:, tt, 128:256], op0=ALU.mult, op1=ALU.mult)
            for ti, tt in tiles:
                nc.vector.scalar_tensor_tensor(out=g4[:, tt, 384:512], in0=g4[:, tt, 384:512], scalar=m32[:, ti:ti + 1], in1=g4[:, tt, 0:128], op0=ALU.mult, op1=ALU.mult)
            for ti, tt in tiles:
                nc.vector.tensor_tensor(out=out_t[gi][1][:, tt, :], in0=g4[:, tt, 128:256], in1=g4[:, tt, 384:512], op=ALU.add)

        def cell_tanh(t):
            gi = t // 4
            tt = t % 4
            nc.scalar.activation(out=g4_t[gi][:, tt, 128:256], in_=out_t[gi][1][:, tt, :], func=ACT.Tanh)

        def outputs_vector(t):
            gi = t // 4
            tt = t % 4
            g4 = g4_t[gi]
            oh, oc, os_ = out_t[gi]
            m = m32[:, t:t + 1]
            nc.vector.scalar_tensor_tensor(out=oh[:, tt, :], in0=g4[:, tt, 128:256], scalar=m, in1=g4[:, tt, 256:384], op0=ALU.mult, op1=ALU.mult)
            nc.vector.scalar_tensor_tensor(
                out=os_[:, :, tt, :], in0=g4[:, tt, 128:256].unsqueeze(1).to_broadcast([P, 2, H]), scalar=m,
                in1=g4[:, tt, 512:768].rearrange("p (k c) -> p k c", k=2), op0=ALU.mult, op1=ALU.mult,
            )

        def store(t, n, which, eng):
            gi = t // 4
            lo = t % 4
            oh, oc, os_ = out_t[gi]
            src = (oh, oc, os_[:, 0], os_[:, 1])[which]
            eng.dma_start(out=outs[which][:, t:t + n, :], in_=src[:, lo:lo + n, :])


        nc.vector.memset(ones[:], 1.0)
        nc.vector.memset(braw[:], 0.0)
        nc.scalar.activation(out=warm[:], in_=ones[:, 0:8], func=ACT.Sigmoid)
        make_identity(nc, ident_f[:])
        make_identity(nc, ident_b[:])
        load_w(0, 1)
        load_w(1, 1)
        nc.sync.dma_start(out=whh_raw[:, 0:4, :], in_=weight_hh.rearrange("(j p) k -> p j k", p=P))
        nc.sync.dma_start(out=whh_raw[:, 4:6, :], in_=weight_sh.rearrange("(j p) k -> p j k", p=P))
        load_w(2, 2)
        nc.sync.dma_start(out=braw[0:1, :], in_=bias_ih.unsqueeze(0))
        nc.sync.dma_start(out=braw[1:2, 0:512], in_=bias_hh.unsqueeze(0))
        nc.sync.dma_start(out=braw[1:2, 512:768], in_=bias_sh.unsqueeze(0))
        load_hs(0, 4)
        load_w(4, 2)
        load_x(0)
        load_x(1)
        load_hs(4, 12)
        load_x(2)
        load_x(3)
        nc.sync.dma_start(out=c_sb[:], in_=cv)
        nc.sync.dma_start(out=m_bf[:], in_=mask.rearrange("(p t) -> p t", t=NT))
        load_x(4)
        load_hs(16, 16)
        load_x(5)
        load_x(6)
        load_x(7)
        load_x(8)
        load_x(9)
        load_x(10)
        load_x(11)
        load_x(12)
        load_x(13)
        load_x(14)
        load_x(15)

        keep_warm(15, "P0")
        w_pe(0, "AC")
        w_ev(0, "V")
        keep_warm(4, "P0")
        w_pe(1, "A0")
        w_ev(1, "V")
        w_quant(0)
        keep_warm(4, "P0")
        wt_ps = psum.tile([P, 6, H], BF16, tag="X0", name="wt_ps")
        for j in range(6):
            nc.tensor.transpose(wt_ps[:, j, :], whh_raw[:, j, :], ident_b[:])
        nc.scalar.copy(out=wT[:], in_=wt_ps[:].rearrange("p j k -> p (j k)"))
        w_pe(2, "A1")
        w_ev(2, "V")
        b_ps0 = psum.tile([P, 512], F32, tag="P0", name="b_ps0")
        nc.tensor.matmul(out=b_ps0[:], lhsT=ones[:], rhs=braw[:, 0:512], start=True, stop=True)
        nc.scalar.copy(out=bias_bc[:, 0:512], in_=b_ps0[:])
        b_ps1 = psum.tile([P, 512], F32, tag="P1", name="b_ps1")
        nc.tensor.matmul(out=b_ps1[:, 0:256], lhsT=ones[:], rhs=braw[:, 512:768], start=True, stop=True)
        nc.scalar.copy(out=bias_bc[:, 512:768], in_=b_ps1[:, 0:256])
        w_pe(3, "X1")
        w_ev(3, "V")
        w_quant(1)
        keep_warm(4, "PC")
        hs_pe(0, "X0")
        hs_ev(0, "S")
        hs_pe(1, "AC")
        hs_ev(1, "S")
        plain_main(0, 0)
        plain_main(0, 1)
        plain_share(0)
        add_bias(0)
        w_pe(4, "A0")
        w_ev(4, "S")
        w_pe(5, "X0")
        w_ev(5, "S")
        w_quant(2)
        x_pe(0, "A1")
        x_ev(0, "S")
        x_pe(1, "X1")
        x_ev(1, "S")
        quantise(0)
        plain_main(1, 0)
        plain_main(1, 1)
        plain_share(1)
        add_bias(1)
        x_pe(2, "X0")
        x_ev(2, "S")
        hs_pe(2, "A1")
        hs_ev(2, "S")
        x_pe(3, "X1")
        x_ev(3, "S")
        mx(0)
        nc.gpsimd.tensor_copy(out=m32[:], in_=m_bf[:])

        units = ([(t, 2, t // 2 + 1) for t in range(0, G_FIRST, 2)] + [(t, 4, t // 2 + 2) for t in range(G_FIRST, G_PAIRED, 4)]
                 + [(t, 2, t // 2 + 1) for t in range(G_PAIRED, G_TILES, 2)])

        def cell_scalars(j):
            for t, n, ready in units:
                for h in range(n // 2):
                    if j == ready + 1 + h:
                        cell_scalar(t + 2 * h)
                        cell_scalar(t + 2 * h + 1)
                        if 2 * h + 2 == n:
                            store(t, n, 1, nc.sync)

        def cell_gpsimd(j):
            for t, n, ready in units:
                gi = t // 4
                if j == ready:
                    if t % 4 == 0:
                        out_tiles(gi)
                    cell_sum_gpsimd(gi, t % 4, n)
                if j == ready + 1 + 0 + n // 2:
                    outputs_gpsimd(gi, t % 4, n)
                    for which in (0, 2, 3):
                        store(t, n, which, nc.sync)

        def outputs_v(k, eng):
            outputs_vector(2 * k)
            outputs_vector(2 * k + 1)
            for which in (0, 2, 3):
                store(2 * k, 2, which, eng)

        last = NPAIR - 1
        for j in range(NPAIR):
            k = j + 2
            if 0 < j < last - 1:
                add_bias(j + 1)
            if j < last:
                quantise(j + 1)
            if j > 0:
                gate_functions(2 * (j - 1), 2)
            if k < NPAIR:
                plain_main(k, 0)
                x_pe(2 * k, "X%d" % (3 * j % 2))
                plain_main(k, 1)
                x_pe(2 * k + 1, "X%d" % ((3 * j + 1) % 2))
                plain_share(k)
            if k < NPAIR:
                x_ev(2 * k, "S")
                x_ev(2 * k + 1, "S")
            if j + 3 < NPAIR:
                hs_pe(j + 3, "X%d" % (3 * j % 2))
            cell_scalars(j)
            if j + 3 < NPAIR:
                hs_ev(j + 3, "S")
            add_mx(j)
            if j < last:
                mx(j + 1)
            if j == last - 1:
                add_bias(j + 1)
            cell_gpsimd(j)
        first = G_TILES // 2
        gate_functions(2 * last, 2)
        for k in range(first, last + 1):
            if k % 2 == 0:
                out_tiles(k // 2)
            cell_vector(2 * k, 2)
            cell_tanh(2 * k)
            cell_tanh(2 * k + 1)
            store(2 * k, 2, 1, nc.sync)
            if k == first:
                for j in range(last, last + 4):
                    cell_scalars(j)
                    cell_gpsimd(j + 1)
            if k - 1 >= first:
                outputs_v(k - 1, nc.sync)
        for k in range(last + 1 - 1, last + 1):
            outputs_v(k, nc.scalar)
